import numpy as np
import ml_dtypes


def mxq(x, axis, fmt="e4m3"):
    dtype, down = {"e4m3": (ml_dtypes.float8_e4m3fn, 7), "e5m2": (ml_dtypes.float8_e5m2, 14)}[fmt]
    v = np.moveaxis(np.asarray(x, np.float32).astype(ml_dtypes.bfloat16).astype(np.float64), axis, -1)
    blocks = v.reshape(v.shape[:-1] + (-1, 32))
    amax = np.abs(blocks).max(-1, keepdims=True)
    byte = np.maximum(np.where(amax > 0, np.frexp(amax)[1] - 1 + 127, 0) - down, 1)
    scale = np.exp2(byte - 127.0)
    codes = (blocks / scale).astype(np.float32).astype(dtype).astype(np.float64)
    return np.moveaxis((codes * scale).reshape(v.shape), -1, axis)


WIDE = False


def mx_kscale(k):
    if not WIDE:
        return np.ones(k)
    levels = np.array([30, -30])
    if k % 512:
        return np.exp2(np.random.permutation(np.resize(levels, k // 32))).repeat(32)
    a = np.empty((k // 512, 16))
    for p in range(k // 512):
        a[p, :8] = np.random.permutation(np.resize(levels, 8))
        for g in range(8):
            far = levels[np.abs(levels - a[p, g]) >= 10]
            a[p, g + 8] = far[np.random.randint(len(far))]
    return np.exp2(a.ravel()).repeat(32)


BF16 = ml_dtypes.bfloat16


def bf(x):
    return np.asarray(x, np.float32).astype(BF16)


def f64(x):
    return np.asarray(x).astype(np.float64)


E2M1 = np.array([0.0, 0.5, 1.0, 1.5, 2.0, 3.0, 4.0, 6.0, -0.0, -0.5, -1.0, -1.5, -2.0, -3.0, -4.0, -6.0])


def pack_weight(w, fmt):
    k, n = w.shape
    w = f64(bf(w)).reshape(k // 32, 32, n)
    amax = np.abs(w).max(1)
    if fmt == "e4m3":
        byte = np.frexp(amax)[1] - 1 + 127 - 7
    else:
        mant, ex = np.frexp(amax / 6.0)
        byte = np.where(mant > 0.5, ex, ex - 1) + 127
    byte = np.clip(np.where(amax > 0, byte, 1), 1, 254)
    scaled = (w * np.exp2(127.0 - byte)[:, None, :]).reshape(k, n).astype(np.float32)
    by_word = np.ascontiguousarray(scaled.reshape(k // 512, 128, 4, n).transpose(0, 1, 3, 2))
    if fmt == "e4m3":
        words = by_word.astype(ml_dtypes.float8_e4m3fn).view(np.uint8)
    else:
        c = by_word.astype(ml_dtypes.float4_e2m1fn).view(np.uint8) & 0xF
        words = c[..., 0::2] | (c[..., 1::2] << 4)
    return np.ascontiguousarray(words), np.ascontiguousarray(byte.astype(np.uint8).reshape(k // 512, 16, n))


def unpack_weight(words, scales, fmt):
    g, p, n, _ = words.shape
    if fmt == "e4m3":
        vals = np.ascontiguousarray(words).view(ml_dtypes.float8_e4m3fn).astype(np.float64)
    else:
        nib = np.empty((g, p, n, 4), np.uint8)
        nib[..., 0::2] = words & 0xF
        nib[..., 1::2] = words >> 4
        vals = E2M1[nib]
    vals = vals * np.repeat(np.exp2(scales.astype(np.float64) - 127.0), 8, axis=1)[..., None]
    return vals.transpose(0, 1, 3, 2).reshape(g * 512, n)

def pack4(w):
    words, scales = pack_weight(w, "e2m1")
    return words.reshape(words.shape[0], 128, -1), scales


def unpack4(words, scales):
    return unpack_weight(words.reshape(words.shape[0], 128, -1, 2), scales, "e2m1")


B, I, H = 1024, 2048, 256


def sigmoid(v):
    return 1.0 / (1.0 + np.exp(-v))


def setup_inputs():
    s = mx_kscale(I)
    input_ = bf(np.random.standard_normal((B, I)) * s)
    c_input = bf(np.random.standard_normal((B, 1, H)))
    h_0 = bf(np.random.standard_normal((B, H)))
    weight_ih_words, weight_ih_scales = pack4(np.random.standard_normal((I, 3 * H)) / np.sqrt(I) / s[:, None])
    weight_hh = bf(np.random.standard_normal((H, 3 * H)) / np.sqrt(H))
    alpha_weight_ih_words, alpha_weight_ih_scales = pack4(np.random.standard_normal((I, H)) / np.sqrt(I) / s[:, None])
    alpha_weight_hh = bf(np.random.standard_normal((H, H)) / np.sqrt(H))
    bias = bf(np.random.standard_normal(3 * H) * 0.5)
    alpha_bias = bf(np.random.standard_normal(H) * 0.5)
    return {
        "input_": input_,
        "c_input": c_input,
        "h_0": h_0,
        "weight_ih_words": weight_ih_words,
        "weight_ih_scales": weight_ih_scales,
        "weight_hh": weight_hh,
        "alpha_weight_ih_words": alpha_weight_ih_words,
        "alpha_weight_ih_scales": alpha_weight_ih_scales,
        "alpha_weight_hh": alpha_weight_hh,
        "bias": bias,
        "alpha_bias": alpha_bias,
    }


def reference(input_, c_input, h_0, weight_ih_words, weight_ih_scales, weight_hh, alpha_weight_ih_words, alpha_weight_ih_scales, alpha_weight_hh, bias, alpha_bias):
    xq = mxq(f64(input_), 1, "e5m2")
    wh_b = f64(h_0) @ f64(weight_hh) + f64(bias)
    wi = xq @ unpack4(weight_ih_words, weight_ih_scales)
    pre = wh_b + wi
    i_gate = sigmoid(pre[:, :H])
    o_gate = sigmoid(pre[:, H:2 * H])
    g = np.tanh(pre[:, 2 * H:])
    c_in = f64(c_input)[:, 0, :]
    alpha = sigmoid((xq @ unpack4(alpha_weight_ih_words, alpha_weight_ih_scales)) + f64(alpha_bias) + c_in @ f64(alpha_weight_hh))
    e_i = np.exp(i_gate)
    e_a = np.exp(alpha)
    denom = e_i + e_a
    w_i = e_i / denom
    w_a = e_a / denom
    c_1 = w_i * g + w_a * c_in
    h_1 = o_gate * np.tanh(c_1)
    return (h_1, c_1)

@@ -1,0 +1,355 @@
+from contextlib import ExitStack
+
+import concourse.mybir as mybir
+from concourse.masks import make_identity
+
+B, I, H = 1024, 2048, 256
+FLOPS = 2 * B * I * 4 * H + 2 * B * H * 4 * H
+
+F32 = mybir.dt.float32
+BF16 = mybir.dt.bfloat16
+I32 = mybir.dt.int32
+U32 = mybir.dt.uint32
+U8 = mybir.dt.uint8
+E5M2X4 = mybir.dt.float8_e5m2_x4
+E2M1X4 = mybir.dt.float4_e2m1fn_x4
+ACT = mybir.ActivationFunctionType
+ALU = mybir.AluOpType
+
+P = 128
+TILES = B // P
+PASSES = I // (4 * P)
+BANK = 512
+HEAD = 4
+LAST = TILES - 1
+
+
+def tile_multiinputlstmcell_pa_kernel(
+    tc, input_, c_input, h_0, weight_ih_words, weight_ih_scales, weight_hh,
+    alpha_weight_ih_words, alpha_weight_ih_scales, alpha_weight_hh, bias, alpha_bias,
+    out_0, out_1,
+):
+    nc = tc.nc
+    x_rows = input_.rearrange("(p i) k -> p i k", i=TILES)
+    h_rows = h_0.rearrange("(p i) d -> p i d", i=TILES)
+    c_rows = c_input.rearrange("(p i) o d -> p i (o d)", i=TILES)
+    h_out = out_0.rearrange("(p i) d -> p i d", i=TILES)
+    c_out = out_1.rearrange("(p i) d -> p i d", i=TILES)
+
+    with ExitStack() as ctx:
+        keep = ctx.enter_context(tc.tile_pool(name="keep", bufs=1))
+        work = ctx.enter_context(tc.tile_pool(name="work", bufs=3))
+        psum = ctx.enter_context(tc.psum_pool(name="psum", bufs=1))
+        ctx.enter_context(tc.manual_schedule())
+
+        ident = keep.tile([P, P], F32, name="ident")
+        ones = keep.tile([P, P], BF16, name="ones")
+        bias_row = keep.tile([P, 4 * H], BF16, name="bias_row")
+        bias_x = keep.tile([P, BANK], F32, name="bias_x")
+        plane_a = keep.tile([P, PASSES, H], U8, name="plane_a", align_bytes=64)
+        plane_w = keep.tile([P, PASSES, 3 * H], U8, name="plane_w", align_bytes=64)
+        words_a = keep.tile([P, PASSES, 2 * H], U8, name="words_a", align_bytes=64)
+        words_i = keep.tile([P, PASSES, 2 * H], U8, name="words_i", align_bytes=64)
+        words_y = keep.tile([P, PASSES, 2 * BANK], U8, name="words_y", align_bytes=64)
+        w_hh = keep.tile([P, 2, 3 * H], BF16, name="w_hh")
+        a_hh = keep.tile([P, 2, H], BF16, name="a_hh")
+        h_sb = [keep.tile([P, HEAD, H], BF16, name="h_sb%d" % j) for j in range(2)]
+        c_sb = [keep.tile([P, HEAD, H], BF16, name="c_sb%d" % j) for j in range(2)]
+        x_sb = [keep.tile([P, I], BF16, name="x_sb%d" % i) for i in range(TILES)]
+
+        make_identity(nc, ident[:])
+        nc.vector.memset(bias_row[:], 0.0)
+        nc.vector.memset(ones[:], 1.0)
+        for plane in (plane_a, plane_w):
+            nc.vector.memset(plane[:].rearrange("p g n -> p (g n)").bitcast(I32), 0)
+
+        def load_scales(queue, plane, scales):
+            for q in range(4):
+                queue.dma_start(
+                    out=plane[32 * q : 32 * q + 4, :, :].bitcast(I32),
+                    in_=scales[:, 4 * q : 4 * q + 4, :].rearrange("g r n -> r g n").bitcast(I32),
+                )
+
+        def load_words(dst, words):
+            nc.sync.dma_start(out=dst.bitcast(I32), in_=words.rearrange("g p n -> p g n").bitcast(I32))
+
+        def load_x(i):
+            nc.sync.dma_start(out=x_sb[i][:], in_=x_rows[:, i, :])
+
+        nc.scalar.dma_start(out=bias_row[0:1, H:], in_=bias.rearrange("(o n) -> o n", o=1))
+        nc.scalar.dma_start(out=bias_row[0:1, :H], in_=alpha_bias.rearrange("(o n) -> o n", o=1))
+        load_scales(nc.gpsimd, plane_a, alpha_weight_ih_scales)
+
+        nc.sync.dma_start(out=h_sb[0][:], in_=h_rows[:, :HEAD, :])
+        nc.sync.dma_start(out=c_sb[0][:], in_=c_rows[:, :HEAD, :])
+        nc.sync.dma_start(out=w_hh[:], in_=weight_hh.rearrange("(p e) n -> p e n", e=2))
+        nc.sync.dma_start(out=a_hh[:], in_=alpha_weight_hh.rearrange("(p e) n -> p e n", e=2))
+        load_x(0)
+        load_scales(nc.sync, plane_w, weight_ih_scales)
+        load_x(1)
+        load_words(words_i[:], weight_ih_words[:, :, : 2 * H])
+        load_words(words_a[:], alpha_weight_ih_words)
+        load_words(words_y[:], weight_ih_words[:, :, 2 * H :])
+        load_x(2)
+        nc.sync.dma_start(out=h_sb[1][:], in_=h_rows[:, HEAD:, :])
+        nc.sync.dma_start(out=c_sb[1][:], in_=c_rows[:, HEAD:, :])
+        for i in range(3, TILES):
+            load_x(i)
+
+        t = {}
+
+        def c_in(i):
+            return c_sb[i // HEAD][:, i % HEAD, :]
+
+        def transposer(out, in_):
+            return lambda: nc.tensor.transpose(out, in_, ident[:])
+
+        def pairs(words):
+            view = words.bitcast(BF16).rearrange("p (r e) -> p r e", e=2)
+            return [view[:, :, e] for e in range(2)]
+
+        def head_transposes(name, src, copy):
+            bank = psum.tile([P, HEAD, P], F32, name="tr", bufs=3)
+            for i in range(HEAD):
+                nc.tensor.transpose(bank[:, i, :], src[:, i, :].bitcast(F32), ident[:])
+            head_t = keep.tile([P, HEAD, P], F32, name=name + "_head")
+            copy(out=head_t[:], in_=bank[:])
+            for i in range(HEAD):
+                t[name + "T", i] = pairs(head_t[:, i, :])
+
+        head_transposes("h", h_sb[0], nc.scalar.copy)
+        bank = psum.tile([P, BANK], F32, name="hc")
+        nc.tensor.matmul(bank[:], ones[:], bias_row[:, :BANK], start=True, stop=True)
+        nc.vector.tensor_copy(out=bias_x[:], in_=bank[:])
+        head_transposes("c", c_sb[0], nc.vector.tensor_copy)
+
+        def x_tiles(s):
+            return [i for i in range(TILES) if min(i - 1, LAST - 2) == s]
+
+        def plain_phase(s):
+            mats, trs = [], []
+            i = s + 2
+            if 0 <= i < TILES:
+                px = psum.tile([P, BANK], F32, name="mx_x" if i == 1 else "plain_x")
+                py = psum.tile([P, BANK], F32, name="mx_y" if i == 1 else "plain_y")
+                t["px", i], t["py", i] = px, py
+                hT, cT = t["hT", i], t["cT", i]
+                mats = [
+                    (py[:], hT[0], w_hh[:, 0, H:], True, False),
+                    (py[:], hT[1], w_hh[:, 1, H:], False, False),
+                    (py[:], ones[:], bias_row[:, BANK:], False, True),
+                    (px[:, H:], hT[0], w_hh[:, 0, :H], True, False),
+                    (px[:, H:], hT[1], w_hh[:, 1, :H], False, True),
+                    (px[:, :H], cT[0], a_hh[:, 0, :], True, False),
+                    (px[:, :H], cT[1], a_hh[:, 1, :], False, True),
+                ]
+            for i in x_tiles(s):
+                words = x_sb[i][:].bitcast(F32)
+                for half in range(2):
+                    if (i, half) == (LAST, 1):
+                        bank = psum.tile([P, 2, 2, P], F32, name="hc")
+                    else:
+                        bank = psum.tile([P, 2, 2, P], F32, name="tr", bufs=3)
+                    t["xt", i, half] = bank
+                    for g in range(2):
+                        base = 2 * P * (2 * half + g)
+                        for u in range(2):
+                            trs.append(transposer(bank[:, g, u, :], words[:, base + u : base + 2 * P : 2]))
+            i = s + 3
+            if HEAD <= i < TILES:
+                bank = psum.tile([P, 2, P], F32, name="hc")
+                t["hc", i] = bank
+                trs.append(transposer(bank[:, 0, :], h_sb[1][:, i - HEAD, :].bitcast(F32)))
+                trs.append(transposer(bank[:, 1, :], c_sb[1][:, i - HEAD, :].bitcast(F32)))
+            share = {0: [0] * 7, 8: [2, 2, 2, 1, 1, 0, 0], 10: [3, 2, 2, 1, 1, 1, 0], 16: [4, 4, 4, 2, 1, 1, 0]}[len(trs)]
+            for (out, lhs, rhs, start, stop), n in zip(mats, share):
+                nc.tensor.matmul(out, lhs, rhs, start=start, stop=stop)
+                for tr in trs[:n]:
+                    tr()
+                trs = trs[n:]
+            for tr in trs:
+                tr()
+
+        def mx_group(i, out, words, plane, col0, ncols, wcol0):
+            codes, scales = t["codes", i], t["scales", i]
+            for g in range(PASSES):
+                nc.tensor.matmul_mx(
+                    out=out,
+                    lhsT=codes[:, P * g : P * (g + 1)].bitcast(E5M2X4),
+                    lhsT_scale=scales[:, P * g : P * (g + 1)],
+                    rhs=words[:, g, 2 * wcol0 : 2 * (wcol0 + ncols)].bitcast(E2M1X4),
+                    rhs_scale=plane[:, g, col0 : col0 + ncols],
+                    start=(g == 0),
+                    stop=(g == PASSES - 1),
+                )
+
+        def mx_x(i):
+            bank = psum.tile([P, BANK], F32, name="plain_x" if i == LAST else "mx_x")
+            t["mx", i] = bank
+            mx_group(i, bank[:, H:], words_i, plane_w, 0, H, 0)
+            mx_group(i, bank[:, :H], words_a, plane_a, 0, H, 0)
+
+        def mx_y(i):
+            bank = psum.tile([P, BANK], F32, name="mx_y")
+            t["my", i] = bank
+            mx_group(i, bank[:], words_y, plane_w, H, BANK, 0)
+
+        def mx_y_part(i, cols, tag, bufs):
+            bank = psum.tile([P, H], F32, name=tag, bufs=bufs)
+            t["my", i, cols] = bank
+            mx_group(i, bank[:], words_y, plane_w, H + cols, H, cols)
+
+        def pre_y_part(i, cols):
+            if ("pre_y", i) not in t:
+                new("pre_y", i, BANK)
+            nc.vector.tensor_tensor(
+                out=t["pre_y", i][:, cols : cols + H], in0=t["my", i, cols][:], in1=t["rec_y", i][:, cols : cols + H], op=ALU.add
+            )
+
+        def copy_xt(i, half):
+            if half == 0:
+                t["grouped", i] = work.tile([P, 2, 2, P, 2], F32, name="grouped", bufs=3, align_bytes=64)
+            nc.scalar.copy(out=t["grouped", i][:, half], in_=t["xt", i, half][:].rearrange("p g u r -> p g r u"))
+
+        def quant(i):
+            codes = work.tile([P, PASSES * P], U32, name="codes", align_bytes=64)
+            scales = work.tile([P, PASSES * P], U8, name="scales", align_bytes=64)
+            t["codes", i], t["scales", i] = codes, scales
+            nc.vector.quantize_mx(
+                out=codes[:].bitcast(E5M2X4),
+                scales=scales[:],
+                in_=t["grouped", i][:].rearrange("p a g r u -> p (a g r u)").bitcast(BF16),
+            )
+
+        def copy_hc(i):
+            hc = work.tile([P, 2, P], F32, name="hc_sb", bufs=2)
+            nc.scalar.copy(out=hc[:], in_=t["hc", i][:])
+            t["hT", i], t["cT", i] = pairs(hc[:, 0, :]), pairs(hc[:, 1, :])
+
+        def new(name, i, width, bufs=3):
+            t[name, i] = work.tile([P, width], F32, name=name, bufs=bufs)
+            return t[name, i]
+
+        def plain_x_out(i):
+            nc.vector.tensor_tensor(out=new("rec_x", i, BANK, 4)[:], in0=t["px", i][:], in1=bias_x[:], op=ALU.add)
+
+        def plain_y_out(i):
+            nc.scalar.copy(out=new("rec_y", i, BANK, 4)[:], in_=t["py", i][:])
+
+        def pre_x(i):
+            nc.vector.tensor_tensor(out=new("pre_x", i, BANK)[:], in0=t["mx", i][:], in1=t["rec_x", i][:], op=ALU.add)
+
+        def pre_y(i):
+            nc.vector.tensor_tensor(out=new("pre_y", i, BANK)[:], in0=t["my", i][:], in1=t["rec_y", i][:], op=ALU.add)
+
+        def gates_x(i):
+            nc.scalar.activation(out=new("gate_x", i, BANK)[:], in_=t["pre_x", i][:], func=ACT.Sigmoid)
+
+        def gate_g(i):
+            nc.scalar.activation(out=new("g", i, H)[:], in_=t["pre_y", i][:, H:], func=ACT.Tanh)
+
+        def gate_o(i):
+            nc.scalar.activation(out=new("o", i, H, 4)[:], in_=t["pre_y", i][:, :H], func=ACT.Sigmoid)
+
+        def diff(i):
+            gx = t["gate_x", i]
+            nc.vector.tensor_tensor(out=new("d", i, H)[:], in0=gx[:, H:], in1=gx[:, :H], op=ALU.subtract)
+
+        def weight(i):
+            nc.scalar.activation(out=new("w", i, H)[:], in_=t["d", i][:], func=ACT.Sigmoid)
+
+        def keep_c(i):
+            nc.vector.scalar_tensor_tensor(
+                out=new("u", i, H)[:], in0=t["w", i][:], scalar=-1.0, in1=c_in(i), op0=ALU.add, op1=ALU.mult
+            )
+
+        def take_g(i):
+            nc.vector.tensor_tensor(out=new("m", i, H)[:], in0=t["w", i][:], in1=t["g", i][:], op=ALU.mult)
+
+        def cell(i):
+            nc.vector.tensor_tensor(out=new("c1", i, H)[:], in0=t["m", i][:], in1=t["u", i][:], op=ALU.subtract)
+            nc.sync.dma_start(out=c_out[:, i, :], in_=t["c1", i][:])
+
+        def tanh_cell(i):
+            nc.scalar.activation(out=new("tc", i, H)[:], in_=t["c1", i][:], func=ACT.Tanh)
+
+        def hidden(i):
+            nc.vector.tensor_tensor(out=new("h1", i, H)[:], in0=t["o", i][:], in1=t["tc", i][:], op=ALU.mult)
+            nc.sync.dma_start(out=h_out[:, i, :], in_=t["h1", i][:])
+
+        def run(fn, i, *args):
+            if 0 <= i < TILES:
+                fn(i, *args)
+
+        for s in range(-2, LAST - 1):
+            plain_phase(s)
+            run(pre_y, s - 1)
+            run(gates_x, s - 1)
+            run(copy_xt, s + 1, 0)
+            run(gate_g, s - 1)
+            run(diff, s - 1)
+            run(cell, s - 2)
+            run(copy_xt, s + 1, 1)
+            run(plain_y_out, s + 2)
+            run(plain_x_out, s + 2)
+            run(quant, s + 1)
+            run(weight, s - 1)
+            if s + 3 >= HEAD:
+                run(copy_hc, s + 3)
+            if s == LAST - 2:
+                copy_xt(LAST, 0)
+                copy_xt(LAST, 1)
+            run(tanh_cell, s - 2)
+            run(gate_o, s - 1)
+            run(mx_x, s + 0)
+            run(mx_y, s + 0)
+            run(pre_x, s + 0)
+            run(keep_c, s - 1)
+            run(take_g, s - 1)
+            run(hidden, s - 2)
+
+        quant(7)
+        mx_x(6)
+        mx_x(7)
+        mx_y(6)
+        mx_y_part(7, H, "plain_y", 1)
+        mx_y_part(7, 0, "tr", 3)
+        pre_y(5)
+        gates_x(5)
+        cell(4)
+        gate_g(5)
+        diff(5)
+        pre_x(6)
+        weight(5)
+        tanh_cell(4)
+        gates_x(6)
+        gate_o(5)
+        keep_c(5)
+        take_g(5)
+        pre_x(7)
+        cell(5)
+        diff(6)
+        gates_x(7)
+        weight(6)
+        tanh_cell(5)
+        hidden(4)
+        pre_y(6)
+        diff(7)
+        gate_g(6)
+        weight(7)
+        pre_y_part(7, H)
+        keep_c(6)
+        take_g(6)
+        gate_g(7)
+        gate_o(6)
+        keep_c(7)
+        cell(6)
+        take_g(7)
+        tanh_cell(6)
+        pre_y_part(7, 0)
+        cell(7)
+        hidden(5)
+        gate_o(7)
+        tanh_cell(7)
+        hidden(6)
+        hidden(7)

@@ -21,6 +21,10 @@ TILES = B // P
 PASSES = I // (4 * P)
 BANK = 512
 HEAD = 4
+SPLIT = [(i, 1) for i in range(3, 7)]
+EARLY_BIAS = ()
+LATE_BIAS = ()
+G_HID = ()
 LAST = TILES - 1
 
 
@@ -46,6 +50,7 @@ def tile_multiinputlstmcell_pa_kernel(
         ones = keep.tile([P, P], BF16, name="ones")
         bias_row = keep.tile([P, 4 * H], BF16, name="bias_row")
         bias_x = keep.tile([P, BANK], F32, name="bias_x")
+        bias_y = keep.tile([P, BANK], F32, name="bias_y")
         plane_a = keep.tile([P, PASSES, H], U8, name="plane_a", align_bytes=64)
         plane_w = keep.tile([P, PASSES, 3 * H], U8, name="plane_w", align_bytes=64)
         words_a = keep.tile([P, PASSES, 2 * H], U8, name="words_a", align_bytes=64)
@@ -78,15 +83,15 @@ def tile_multiinputlstmcell_pa_kernel(
 
         nc.scalar.dma_start(out=bias_row[0:1, H:], in_=bias.rearrange("(o n) -> o n", o=1))
         nc.scalar.dma_start(out=bias_row[0:1, :H], in_=alpha_bias.rearrange("(o n) -> o n", o=1))
-        load_scales(nc.gpsimd, plane_a, alpha_weight_ih_scales)
 
         nc.sync.dma_start(out=h_sb[0][:], in_=h_rows[:, :HEAD, :])
         nc.sync.dma_start(out=c_sb[0][:], in_=c_rows[:, :HEAD, :])
         nc.sync.dma_start(out=w_hh[:], in_=weight_hh.rearrange("(p e) n -> p e n", e=2))
         nc.sync.dma_start(out=a_hh[:], in_=alpha_weight_hh.rearrange("(p e) n -> p e n", e=2))
         load_x(0)
-        load_scales(nc.sync, plane_w, weight_ih_scales)
+        load_scales(nc.sync, plane_a, alpha_weight_ih_scales)
         load_x(1)
+        load_scales(nc.sync, plane_w, weight_ih_scales)
         load_words(words_i[:], weight_ih_words[:, :, : 2 * H])
         load_words(words_a[:], alpha_weight_ih_words)
         load_words(words_y[:], weight_ih_words[:, :, 2 * H :])
@@ -108,43 +113,65 @@ def tile_multiinputlstmcell_pa_kernel(
             view = words.bitcast(BF16).rearrange("p (r e) -> p r e", e=2)
             return [view[:, :, e] for e in range(2)]
 
-        def head_transposes(name, src, copy):
-            bank = psum.tile([P, HEAD, P], F32, name="tr", bufs=3)
-            for i in range(HEAD):
-                nc.tensor.transpose(bank[:, i, :], src[:, i, :].bitcast(F32), ident[:])
-            head_t = keep.tile([P, HEAD, P], F32, name=name + "_head")
+        def head_transposes(name, src, tiles, copy):
+            bank = psum.tile([P, len(tiles), P], F32, name="tr", bufs=3)
+            for j, i in enumerate(tiles):
+                nc.tensor.transpose(bank[:, j, :], src[:, i, :].bitcast(F32), ident[:])
+            head_t = keep.tile([P, len(tiles), P], F32, name="%s_head%d" % (name, tiles[0]))
             copy(out=head_t[:], in_=bank[:])
-            for i in range(HEAD):
-                t[name + "T", i] = pairs(head_t[:, i, :])
+            for j, i in enumerate(tiles):
+                t[name + "T", i] = pairs(head_t[:, j, :])
 
-        head_transposes("h", h_sb[0], nc.scalar.copy)
-        bank = psum.tile([P, BANK], F32, name="hc")
-        nc.tensor.matmul(bank[:], ones[:], bias_row[:, :BANK], start=True, stop=True)
-        nc.vector.tensor_copy(out=bias_x[:], in_=bank[:])
-        head_transposes("c", c_sb[0], nc.vector.tensor_copy)
+        def plain_banks(i):
+            t["px", i] = psum.tile([P, BANK], F32, name="mx_x" if i == 1 else "plain_x")
+            t["py", i] = psum.tile([P, BANK], F32, name="mx_y" if i == 1 else "plain_y")
+
+        def spread_bias(dst, cols):
+            bank = psum.tile([P, BANK], F32, name="hc")
+            nc.tensor.matmul(bank[:], ones[:], bias_row[:, cols], start=True, stop=True)
+            nc.vector.tensor_copy(out=dst[:], in_=bank[:])
+
+        head_transposes("h", h_sb[0], range(HEAD), nc.scalar.copy)
+        spread_bias(bias_x, slice(0, BANK))
+        head_transposes("c", c_sb[0], range(HEAD), nc.scalar.copy)
+
+        def split_words(i, half):
+            words = x_sb[i][:, I // 2 * half : I // 2 * (half + 1)].bitcast(F32)
+            if (i, half) not in SPLIT:
+                t["xp", i, half] = words.rearrange("p (g m u) -> p g u m", g=2, u=2)
+                return
+            xp = work.tile([P, 2, 2, P], F32, name="xp%d" % half, bufs=2)
+            t["xp", i, half] = xp
+            copy = nc.vector.tensor_copy if i < 2 else nc.scalar.copy
+            copy(out=xp[:], in_=words.rearrange("p (g m u) -> p g u m", g=2, u=2))
 
         def x_tiles(s):
             return [i for i in range(TILES) if min(i - 1, LAST - 2) == s]
 
         def plain_phase(s):
+            for i in x_tiles(s):
+                for half in range(2):
+                    if (i, half) not in SPLIT:
+                        split_words(i, half)
             mats, trs = [], []
             i = s + 2
             if 0 <= i < TILES:
-                px = psum.tile([P, BANK], F32, name="mx_x" if i == 1 else "plain_x")
-                py = psum.tile([P, BANK], F32, name="mx_y" if i == 1 else "plain_y")
-                t["px", i], t["py", i] = px, py
-                hT, cT = t["hT", i], t["cT", i]
+                if i not in EARLY_BIAS:
+                    plain_banks(i)
+                px, py = t["px", i], t["py", i]
+                hT = t["hT", i]
                 mats = [
-                    (py[:], hT[0], w_hh[:, 0, H:], True, False),
-                    (py[:], hT[1], w_hh[:, 1, H:], False, False),
-                    (py[:], ones[:], bias_row[:, BANK:], False, True),
-                    (px[:, H:], hT[0], w_hh[:, 0, :H], True, False),
-                    (px[:, H:], hT[1], w_hh[:, 1, :H], False, True),
-                    (px[:, :H], cT[0], a_hh[:, 0, :], True, False),
-                    (px[:, :H], cT[1], a_hh[:, 1, :], False, True),
+                    (py[:], hT[0], w_hh[:, 0, H:], i not in EARLY_BIAS, False),
+                    (py[:], hT[1], w_hh[:, 1, H:], False, i not in LATE_BIAS),
                 ]
+                if i in LATE_BIAS:
+                    mats.append((py[:], ones[:], bias_row[:, BANK:], False, True))
+                mats.append((px[:, H:], hT[0], w_hh[:, 0, :H], True, False))
+                mats.append((px[:, H:], hT[1], w_hh[:, 1, :H], False, True))
+                cT = t["cT", i]
+                mats.append((px[:, :H], cT[0], a_hh[:, 0, :], True, False))
+                mats.append((px[:, :H], cT[1], a_hh[:, 1, :], False, True))
             for i in x_tiles(s):
-                words = x_sb[i][:].bitcast(F32)
                 for half in range(2):
                     if (i, half) == (LAST, 1):
                         bank = psum.tile([P, 2, 2, P], F32, name="hc")
@@ -152,16 +179,16 @@ def tile_multiinputlstmcell_pa_kernel(
                         bank = psum.tile([P, 2, 2, P], F32, name="tr", bufs=3)
                     t["xt", i, half] = bank
                     for g in range(2):
-                        base = 2 * P * (2 * half + g)
                         for u in range(2):
-                            trs.append(transposer(bank[:, g, u, :], words[:, base + u : base + 2 * P : 2]))
+                            trs.append(transposer(bank[:, g, u, :], t["xp", i, half][:, g, u, :]))
             i = s + 3
             if HEAD <= i < TILES:
                 bank = psum.tile([P, 2, P], F32, name="hc")
                 t["hc", i] = bank
                 trs.append(transposer(bank[:, 0, :], h_sb[1][:, i - HEAD, :].bitcast(F32)))
                 trs.append(transposer(bank[:, 1, :], c_sb[1][:, i - HEAD, :].bitcast(F32)))
-            share = {0: [0] * 7, 8: [2, 2, 2, 1, 1, 0, 0], 10: [3, 2, 2, 1, 1, 1, 0], 16: [4, 4, 4, 2, 1, 1, 0]}[len(trs)]
+            gaps = max(len(mats) - 1, 1)
+            share = [len(trs) // gaps + (j < len(trs) % gaps) for j in range(gaps)] + [0]
             for (out, lhs, rhs, start, stop), n in zip(mats, share):
                 nc.tensor.matmul(out, lhs, rhs, start=start, stop=stop)
                 for tr in trs[:n]:
@@ -169,6 +196,8 @@ def tile_multiinputlstmcell_pa_kernel(
                 trs = trs[n:]
             for tr in trs:
                 tr()
+            if s == -2:
+                spread_bias(bias_y, slice(BANK, 2 * BANK))
 
         def mx_group(i, out, words, plane, col0, ncols, wcol0):
             codes, scales = t["codes", i], t["scales", i]
@@ -234,7 +263,10 @@ def tile_multiinputlstmcell_pa_kernel(
             nc.vector.tensor_tensor(out=new("rec_x", i, BANK, 4)[:], in0=t["px", i][:], in1=bias_x[:], op=ALU.add)
 
         def plain_y_out(i):
-            nc.scalar.copy(out=new("rec_y", i, BANK, 4)[:], in_=t["py", i][:])
+            if i in EARLY_BIAS or i in LATE_BIAS:
+                nc.scalar.copy(out=new("rec_y", i, BANK, 4)[:], in_=t["py", i][:])
+            else:
+                nc.vector.tensor_tensor(out=new("rec_y", i, BANK, 4)[:], in0=t["py", i][:], in1=bias_y[:], op=ALU.add)
 
         def pre_x(i):
             nc.vector.tensor_tensor(out=new("pre_x", i, BANK)[:], in0=t["mx", i][:], in1=t["rec_x", i][:], op=ALU.add)
@@ -274,31 +306,39 @@ def tile_multiinputlstmcell_pa_kernel(
             nc.scalar.activation(out=new("tc", i, H)[:], in_=t["c1", i][:], func=ACT.Tanh)
 
         def hidden(i):
-            nc.vector.tensor_tensor(out=new("h1", i, H)[:], in0=t["o", i][:], in1=t["tc", i][:], op=ALU.mult)
+            (nc.gpsimd if i in G_HID else nc.vector).tensor_tensor(out=new("h1", i, H)[:], in0=t["o", i][:], in1=t["tc", i][:], op=ALU.mult)
             nc.sync.dma_start(out=h_out[:, i, :], in_=t["h1", i][:])
 
         def run(fn, i, *args):
             if 0 <= i < TILES:
                 fn(i, *args)
 
-        for s in range(-2, LAST - 1):
+        for s in range(-2, LAST - 2):
             plain_phase(s)
+            if s < 0:
+                for half in range(2):
+                    if (s + 2, half) in SPLIT:
+                        split_words(s + 2, half)
             run(pre_y, s - 1)
             run(gates_x, s - 1)
             run(copy_xt, s + 1, 0)
+            run(plain_y_out, s + 2)
             run(gate_g, s - 1)
             run(diff, s - 1)
             run(cell, s - 2)
             run(copy_xt, s + 1, 1)
-            run(plain_y_out, s + 2)
             run(plain_x_out, s + 2)
             run(quant, s + 1)
+            if s >= 0 and (s + 2, 0) in SPLIT:
+                split_words(s + 2, 0)
             run(weight, s - 1)
             if s + 3 >= HEAD:
                 run(copy_hc, s + 3)
             if s == LAST - 2:
                 copy_xt(LAST, 0)
                 copy_xt(LAST, 1)
+            if s >= 0 and (s + 2, 1) in SPLIT:
+                split_words(s + 2, 1)
             run(tanh_cell, s - 2)
             run(gate_o, s - 1)
             run(mx_x, s + 0)
@@ -308,48 +348,70 @@ def tile_multiinputlstmcell_pa_kernel(
             run(take_g, s - 1)
             run(hidden, s - 2)
 
+        plain_phase(5)
+        pre_y(4)
+        gates_x(4)
+        copy_xt(6, 0)
+        diff(4)
+        cell(3)
+        gate_g(4)
+        weight(4)
+        copy_xt(6, 1)
+        plain_y_out(7)
+        tanh_cell(3)
+        copy_xt(7, 0)
+        copy_xt(7, 1)
+        keep_c(4)
+        take_g(4)
+        hidden(3)
+        plain_x_out(7)
+        quant(6)
+        gate_o(4)
+        mx_x(5)
+        mx_y(5)
+        pre_x(5)
         quant(7)
         mx_x(6)
         mx_x(7)
         mx_y(6)
         mx_y_part(7, H, "plain_y", 1)
         mx_y_part(7, 0, "tr", 3)
-        pre_y(5)
         gates_x(5)
         cell(4)
-        gate_g(5)
-        diff(5)
-        pre_x(6)
-        weight(5)
+        pre_y(5)
         tanh_cell(4)
+        diff(5)
+        gate_g(5)
+        weight(5)
+        pre_x(6)
         gates_x(6)
-        gate_o(5)
+        hidden(4)
         keep_c(5)
         take_g(5)
         pre_x(7)
-        cell(5)
-        diff(6)
+        gate_o(5)
         gates_x(7)
+        diff(6)
+        cell(5)
         weight(6)
-        tanh_cell(5)
-        hidden(4)
         pre_y(6)
+        tanh_cell(5)
         diff(7)
         gate_g(6)
         weight(7)
         pre_y_part(7, H)
+        gate_g(7)
         keep_c(6)
         take_g(6)
-        gate_g(7)
+        pre_y_part(7, 0)
         gate_o(6)
         keep_c(7)
         cell(6)
         take_g(7)
-        tanh_cell(6)
-        pre_y_part(7, 0)
-        cell(7)
-        hidden(5)
         gate_o(7)
+        tanh_cell(6)
+        hidden(5)
+        cell(7)
         tanh_cell(7)
         hidden(6)
         hidden(7)

@@ -21,10 +21,11 @@ TILES = B // P
 PASSES = I // (4 * P)
 BANK = 512
 HEAD = 4
-SPLIT = [(i, 1) for i in range(3, 7)]
+SPLIT = [(i, 1) for i in range(3, 8)]
 EARLY_BIAS = ()
 LATE_BIAS = ()
-G_HID = ()
+G_TILES = {"d": range(2, 7), "u": range(7), "m": range(7), "c1": range(7), "h1": range(0)}
+V_COPY = range(2, 7)
 LAST = TILES - 1
 
 
@@ -96,15 +97,13 @@ def tile_multiinputlstmcell_pa_kernel(
         load_words(words_a[:], alpha_weight_ih_words)
         load_words(words_y[:], weight_ih_words[:, :, 2 * H :])
         load_x(2)
+        load_x(3)
         nc.sync.dma_start(out=h_sb[1][:], in_=h_rows[:, HEAD:, :])
         nc.sync.dma_start(out=c_sb[1][:], in_=c_rows[:, HEAD:, :])
-        for i in range(3, TILES):
+        for i in range(4, TILES):
             load_x(i)
 
         t = {}
-
-        def c_in(i):
-            return c_sb[i // HEAD][:, i % HEAD, :]
 
         def transposer(out, in_):
             return lambda: nc.tensor.transpose(out, in_, ident[:])
@@ -142,21 +141,20 @@ def tile_multiinputlstmcell_pa_kernel(
                 return
             xp = work.tile([P, 2, 2, P], F32, name="xp%d" % half, bufs=2)
             t["xp", i, half] = xp
-            copy = nc.vector.tensor_copy if i < 2 else nc.scalar.copy
-            copy(out=xp[:], in_=words.rearrange("p (g m u) -> p g u m", g=2, u=2))
+            nc.scalar.copy(out=xp[:], in_=words.rearrange("p (g m u) -> p g u m", g=2, u=2))
 
         def x_tiles(s):
-            return [i for i in range(TILES) if min(i - 1, LAST - 2) == s]
+            return [i for i in range(TILES) if i - 1 == s]
 
-        def plain_phase(s):
+        def plain_phase(s, part=None):
             for i in x_tiles(s):
                 for half in range(2):
                     if (i, half) not in SPLIT:
                         split_words(i, half)
             mats, trs = [], []
-            i = s + 2
-            if 0 <= i < TILES:
-                if i not in EARLY_BIAS:
+            i = s + 2 if s <= 0 else s
+            if i < 3 and s <= 0 or 3 <= i < TILES:
+                if ("px", i) not in t:
                     plain_banks(i)
                 px, py = t["px", i], t["py", i]
                 hT = t["hT", i]
@@ -171,22 +169,22 @@ def tile_multiinputlstmcell_pa_kernel(
                 cT = t["cT", i]
                 mats.append((px[:, :H], cT[0], a_hh[:, 0, :], True, False))
                 mats.append((px[:, :H], cT[1], a_hh[:, 1, :], False, True))
+            if part is not None:
+                mats = mats[-4:] if part == "x" else mats[:-4]
             for i in x_tiles(s):
                 for half in range(2):
-                    if (i, half) == (LAST, 1):
-                        bank = psum.tile([P, 2, 2, P], F32, name="hc")
-                    else:
-                        bank = psum.tile([P, 2, 2, P], F32, name="tr", bufs=3)
+                    bank = psum.tile([P, 2, 2, P], F32, name="tr", bufs=3)
                     t["xt", i, half] = bank
                     for g in range(2):
                         for u in range(2):
                             trs.append(transposer(bank[:, g, u, :], t["xp", i, half][:, g, u, :]))
-            i = s + 3
-            if HEAD <= i < TILES:
-                bank = psum.tile([P, 2, P], F32, name="hc")
+            i = s + 1
+            if HEAD <= i < TILES and i % 2 == 0:
+                bank = psum.tile([P, 2, 2, P], F32, name="hc")
                 t["hc", i] = bank
-                trs.append(transposer(bank[:, 0, :], h_sb[1][:, i - HEAD, :].bitcast(F32)))
-                trs.append(transposer(bank[:, 1, :], c_sb[1][:, i - HEAD, :].bitcast(F32)))
+                for j in range(2):
+                    trs.append(transposer(bank[:, j, 0, :], h_sb[1][:, i + j - HEAD, :].bitcast(F32)))
+                    trs.append(transposer(bank[:, j, 1, :], c_sb[1][:, i + j - HEAD, :].bitcast(F32)))
             gaps = max(len(mats) - 1, 1)
             share = [len(trs) // gaps + (j < len(trs) % gaps) for j in range(gaps)] + [0]
             for (out, lhs, rhs, start, stop), n in zip(mats, share):
@@ -213,7 +211,7 @@ def tile_multiinputlstmcell_pa_kernel(
                 )
 
         def mx_x(i):
-            bank = psum.tile([P, BANK], F32, name="plain_x" if i == LAST else "mx_x")
+            bank = psum.tile([P, BANK], F32, name="mx_x")
             t["mx", i] = bank
             mx_group(i, bank[:, H:], words_i, plane_w, 0, H, 0)
             mx_group(i, bank[:, :H], words_a, plane_a, 0, H, 0)
@@ -223,22 +221,44 @@ def tile_multiinputlstmcell_pa_kernel(
             t["my", i] = bank
             mx_group(i, bank[:], words_y, plane_w, H, BANK, 0)
 
+        def mx_x_part(i, cols, words, plane, tag, bufs):
+            bank = psum.tile([P, H], F32, name=tag, bufs=bufs)
+            t["mx", i, cols] = bank
+            mx_group(i, bank[:], words, plane, 0, H, 0)
+
+        def pre_x_part(i, cols):
+            nc.vector.tensor_tensor(
+                out=buf("pre_x", i, 1, BANK)[:, 0, cols : cols + H],
+                in0=t["mx", i, cols][:],
+                in1=t["rec_x", i][:, cols : cols + H],
+                op=ALU.add,
+            )
+
+        def gates_x_part(i, cols):
+            nc.scalar.activation(
+                out=buf("gate_x", i, 1, BANK)[:, 0, cols : cols + H],
+                in_=buf("pre_x", i, 1, BANK)[:, 0, cols : cols + H],
+                func=ACT.Sigmoid,
+            )
+
         def mx_y_part(i, cols, tag, bufs):
             bank = psum.tile([P, H], F32, name=tag, bufs=bufs)
             t["my", i, cols] = bank
             mx_group(i, bank[:], words_y, plane_w, H + cols, H, cols)
 
         def pre_y_part(i, cols):
-            if ("pre_y", i) not in t:
-                new("pre_y", i, BANK)
             nc.vector.tensor_tensor(
-                out=t["pre_y", i][:, cols : cols + H], in0=t["my", i, cols][:], in1=t["rec_y", i][:, cols : cols + H], op=ALU.add
+                out=buf("pre_y", i, 1, BANK)[:, 0, cols : cols + H],
+                in0=t["my", i, cols][:],
+                in1=t["rec_y", i][:, cols : cols + H],
+                op=ALU.add,
             )
 
         def copy_xt(i, half):
             if half == 0:
                 t["grouped", i] = work.tile([P, 2, 2, P, 2], F32, name="grouped", bufs=3, align_bytes=64)
-            nc.scalar.copy(out=t["grouped", i][:, half], in_=t["xt", i, half][:].rearrange("p g u r -> p g r u"))
+            copy = nc.vector.tensor_copy if half == 0 and i in V_COPY else nc.scalar.copy
+            copy(out=t["grouped", i][:, half], in_=t["xt", i, half][:].rearrange("p g u r -> p g r u"))
 
         def quant(i):
             codes = work.tile([P, PASSES * P], U32, name="codes", align_bytes=64)
@@ -251,9 +271,10 @@ def tile_multiinputlstmcell_pa_kernel(
             )
 
         def copy_hc(i):
-            hc = work.tile([P, 2, P], F32, name="hc_sb", bufs=2)
+            hc = work.tile([P, 2, 2, P], F32, name="hc_sb", bufs=2)
             nc.scalar.copy(out=hc[:], in_=t["hc", i][:])
-            t["hT", i], t["cT", i] = pairs(hc[:, 0, :]), pairs(hc[:, 1, :])
+            for j in range(2):
+                t["hT", i + j], t["cT", i + j] = pairs(hc[:, j, 0, :]), pairs(hc[:, j, 1, :])
 
         def new(name, i, width, bufs=3):
             t[name, i] = work.tile([P, width], F32, name=name, bufs=bufs)
@@ -268,150 +289,129 @@ def tile_multiinputlstmcell_pa_kernel(
             else:
                 nc.vector.tensor_tensor(out=new("rec_y", i, BANK, 4)[:], in0=t["py", i][:], in1=bias_y[:], op=ALU.add)
 
+        def eng(name, i):
+            return nc.gpsimd if i in G_TILES[name] else nc.vector
+
+        def buf(name, i, n, width=H):
+            key = name, i // 2
+            if key not in t:
+                t[key] = work.tile([P, 2, width], F32, name=name, bufs=2)
+            return t[key][:, i % 2 : i % 2 + n, :]
+
         def pre_x(i):
-            nc.vector.tensor_tensor(out=new("pre_x", i, BANK)[:], in0=t["mx", i][:], in1=t["rec_x", i][:], op=ALU.add)
+            nc.vector.tensor_tensor(out=buf("pre_x", i, 1, BANK)[:, 0, :], in0=t["mx", i][:], in1=t["rec_x", i][:], op=ALU.add)
 
         def pre_y(i):
-            nc.vector.tensor_tensor(out=new("pre_y", i, BANK)[:], in0=t["my", i][:], in1=t["rec_y", i][:], op=ALU.add)
+            nc.vector.tensor_tensor(out=buf("pre_y", i, 1, BANK)[:, 0, :], in0=t["my", i][:], in1=t["rec_y", i][:], op=ALU.add)
 
-        def gates_x(i):
-            nc.scalar.activation(out=new("gate_x", i, BANK)[:], in_=t["pre_x", i][:], func=ACT.Sigmoid)
+        def gates_x(i, n):
+            nc.scalar.activation(out=buf("gate_x", i, n, BANK), in_=buf("pre_x", i, n, BANK), func=ACT.Sigmoid)
 
-        def gate_g(i):
-            nc.scalar.activation(out=new("g", i, H)[:], in_=t["pre_y", i][:, H:], func=ACT.Tanh)
+        def gate_g(i, n):
+            nc.scalar.activation(out=buf("g", i, n), in_=buf("pre_y", i, n, BANK)[:, :, H:], func=ACT.Tanh)
 
-        def gate_o(i):
-            nc.scalar.activation(out=new("o", i, H, 4)[:], in_=t["pre_y", i][:, :H], func=ACT.Sigmoid)
+        def gate_o(i, n):
+            nc.scalar.activation(out=buf("o", i, n), in_=buf("pre_y", i, n, BANK)[:, :, :H], func=ACT.Sigmoid)
 
-        def diff(i):
-            gx = t["gate_x", i]
-            nc.vector.tensor_tensor(out=new("d", i, H)[:], in0=gx[:, H:], in1=gx[:, :H], op=ALU.subtract)
+        def diff(i, n):
+            gx = buf("gate_x", i, n, BANK)
+            eng("d", i).tensor_tensor(out=buf("d", i, n), in0=gx[:, :, H:], in1=gx[:, :, :H], op=ALU.subtract)
 
-        def weight(i):
-            nc.scalar.activation(out=new("w", i, H)[:], in_=t["d", i][:], func=ACT.Sigmoid)
+        def weight(i, n):
+            nc.scalar.activation(out=buf("w", i, n), in_=buf("d", i, n), func=ACT.Sigmoid)
 
-        def keep_c(i):
-            nc.vector.scalar_tensor_tensor(
-                out=new("u", i, H)[:], in0=t["w", i][:], scalar=-1.0, in1=c_in(i), op0=ALU.add, op1=ALU.mult
-            )
+        def c_in(i, n):
+            return c_sb[i // HEAD][:, i % HEAD : i % HEAD + n, :]
 
-        def take_g(i):
-            nc.vector.tensor_tensor(out=new("m", i, H)[:], in0=t["w", i][:], in1=t["g", i][:], op=ALU.mult)
+        def keep_c(i, n):
+            eng("u", i).tensor_tensor(out=buf("u", i, n), in0=buf("g", i, n), in1=c_in(i, n), op=ALU.subtract)
 
-        def cell(i):
-            nc.vector.tensor_tensor(out=new("c1", i, H)[:], in0=t["m", i][:], in1=t["u", i][:], op=ALU.subtract)
-            nc.sync.dma_start(out=c_out[:, i, :], in_=t["c1", i][:])
+        def take_g(i, n):
+            eng("m", i).tensor_tensor(out=buf("m", i, n), in0=buf("w", i, n), in1=buf("u", i, n), op=ALU.mult)
 
-        def tanh_cell(i):
-            nc.scalar.activation(out=new("tc", i, H)[:], in_=t["c1", i][:], func=ACT.Tanh)
+        def cell(i, n):
+            eng("c1", i).tensor_tensor(out=buf("c1", i, n), in0=buf("m", i, n), in1=c_in(i, n), op=ALU.add)
+            nc.sync.dma_start(out=c_out[:, i : i + n, :], in_=buf("c1", i, n))
 
-        def hidden(i):
-            (nc.gpsimd if i in G_HID else nc.vector).tensor_tensor(out=new("h1", i, H)[:], in0=t["o", i][:], in1=t["tc", i][:], op=ALU.mult)
-            nc.sync.dma_start(out=h_out[:, i, :], in_=t["h1", i][:])
+        def tanh_cell(i, n):
+            nc.scalar.activation(out=buf("tc", i, n), in_=buf("c1", i, n), func=ACT.Tanh)
+
+        def hidden(i, n):
+            eng("h1", i).tensor_tensor(out=buf("h1", i, n), in0=buf("o", i, n), in1=buf("tc", i, n), op=ALU.mult)
+            nc.sync.dma_start(out=h_out[:, i : i + n, :], in_=buf("h1", i, n))
+
+        def split(i):
+            for half in range(2):
+                if (i, half) in SPLIT:
+                    split_words(i, half)
+
+        def plain_tile(s):
+            return s + 2 if s <= 0 else (s if s >= 3 else -1)
 
         def run(fn, i, *args):
             if 0 <= i < TILES:
                 fn(i, *args)
 
-        for s in range(-2, LAST - 2):
+        for s in range(-2, 7):
             plain_phase(s)
-            if s < 0:
-                for half in range(2):
-                    if (s + 2, half) in SPLIT:
-                        split_words(s + 2, half)
             run(pre_y, s - 1)
-            run(gates_x, s - 1)
+            run(gates_x, s - 1, 1)
+            run(cell, s - 2, 1)
             run(copy_xt, s + 1, 0)
-            run(plain_y_out, s + 2)
-            run(gate_g, s - 1)
-            run(diff, s - 1)
-            run(cell, s - 2)
+            run(gate_g, s - 1, 1)
+            run(diff, s - 1, 1)
             run(copy_xt, s + 1, 1)
-            run(plain_x_out, s + 2)
-            run(quant, s + 1)
-            if s >= 0 and (s + 2, 0) in SPLIT:
-                split_words(s + 2, 0)
-            run(weight, s - 1)
-            if s + 3 >= HEAD:
-                run(copy_hc, s + 3)
-            if s == LAST - 2:
-                copy_xt(LAST, 0)
-                copy_xt(LAST, 1)
-            if s >= 0 and (s + 2, 1) in SPLIT:
-                split_words(s + 2, 1)
-            run(tanh_cell, s - 2)
-            run(gate_o, s - 1)
+            run(keep_c, s - 1, 1)
+            run(plain_y_out, plain_tile(s))
+            if s < 0: run(quant, s + 1)
+            run(plain_x_out, plain_tile(s))
+            run(weight, s - 1, 1)
+            if s >= 0: run(quant, s + 1)
+            if ("hc", s + 1) in t: copy_hc(s + 1)
+            run(tanh_cell, s - 2, 1)
+            run(take_g, s - 1, 1)
+            run(split, s + 2)
+            run(gate_o, s - 1, 1)
             run(mx_x, s + 0)
             run(mx_y, s + 0)
             run(pre_x, s + 0)
-            run(keep_c, s - 1)
-            run(take_g, s - 1)
-            run(hidden, s - 2)
+            if s % 2 == 1: run(hidden, s - 3, 2)
 
-        plain_phase(5)
-        pre_y(4)
-        gates_x(4)
-        copy_xt(6, 0)
-        diff(4)
-        cell(3)
-        gate_g(4)
-        weight(4)
-        copy_xt(6, 1)
-        plain_y_out(7)
-        tanh_cell(3)
-        copy_xt(7, 0)
-        copy_xt(7, 1)
-        keep_c(4)
-        take_g(4)
-        hidden(3)
-        plain_x_out(7)
-        quant(6)
-        gate_o(4)
-        mx_x(5)
-        mx_y(5)
-        pre_x(5)
-        quant(7)
-        mx_x(6)
-        mx_x(7)
-        mx_y(6)
-        mx_y_part(7, H, "plain_y", 1)
-        mx_y_part(7, 0, "tr", 3)
-        gates_x(5)
-        cell(4)
-        pre_y(5)
-        tanh_cell(4)
-        diff(5)
-        gate_g(5)
-        weight(5)
-        pre_x(6)
-        gates_x(6)
-        hidden(4)
-        keep_c(5)
-        take_g(5)
-        pre_x(7)
-        gate_o(5)
-        gates_x(7)
-        diff(6)
-        cell(5)
-        weight(6)
+        hidden(4, 1)
+        plain_phase(7, "x")
+        gates_x(6, 1)
         pre_y(6)
-        tanh_cell(5)
-        diff(7)
-        gate_g(6)
-        weight(7)
+        cell(5, 1)
+        plain_x_out(7)
+        gate_g(6, 1)
+        diff(6, 1)
+        keep_c(6, 1)
+        mx_x_part(7, H, words_i, plane_w, "mx_x", 1)
+        mx_x_part(7, 0, words_a, plane_a, "hc", 1)
+        plain_phase(7, "y")
+        mx_y_part(7, H, "mx_y", 1)
+        mx_y_part(7, 0, "tr", 3)
+        pre_x_part(7, H)
+        weight(6, 1)
+        gates_x_part(7, H)
+        pre_x_part(7, 0)
+        gates_x_part(7, 0)
+        take_g(6, 1)
+        plain_y_out(7)
+        tanh_cell(5, 1)
+        diff(7, 1)
         pre_y_part(7, H)
-        gate_g(7)
-        keep_c(6)
-        take_g(6)
+        weight(7, 1)
+        gate_g(7, 1)
+        cell(6, 1)
+        hidden(5, 1)
+        keep_c(7, 1)
+        gate_o(6, 1)
+        tanh_cell(6, 1)
         pre_y_part(7, 0)
-        gate_o(6)
-        keep_c(7)
-        cell(6)
-        take_g(7)
-        gate_o(7)
-        tanh_cell(6)
-        hidden(5)
-        cell(7)
-        tanh_cell(7)
-        hidden(6)
-        hidden(7)
+        take_g(7, 1)
+        gate_o(7, 1)
+        cell(7, 1)
+        hidden(6, 1)
+        tanh_cell(7, 1)
+        hidden(7, 1)

@@ -18,15 +18,21 @@ ALU = mybir.AluOpType
 
 P = 128
 TILES = B // P
-PASSES = I // (4 * P)
-BANK = 512
-HEAD = 4
-SPLIT = [(i, 1) for i in range(3, 8)]
-EARLY_BIAS = ()
-LATE_BIAS = ()
-G_TILES = {"d": range(2, 7), "u": range(7), "m": range(7), "c1": range(7), "h1": range(0)}
-V_COPY = range(2, 7)
 LAST = TILES - 1
+PASSES = I // (4 * P)
+BANK = 2 * H
+ALPHA, GATE_I = slice(0, H), slice(H, BANK)
+GATE_O, GATE_G = slice(0, H), slice(H, BANK)
+WHOLE = slice(0, BANK)
+
+STATE_HEAD = TILES // 2
+PLAIN_HEAD = 3
+TR_BANKS = 3
+
+PRESORTED = range(PLAIN_HEAD, TILES)
+FIRST_BANK_ON_VECTOR = range(2, LAST)
+DIFF_ON_GPSIMD = range(2, TILES)
+CELL_ON_GPSIMD = range(LAST - 1)
 
 
 def tile_multiinputlstmcell_pa_kernel(
@@ -40,6 +46,8 @@ def tile_multiinputlstmcell_pa_kernel(
     c_rows = c_input.rearrange("(p i) o d -> p i (o d)", i=TILES)
     h_out = out_0.rearrange("(p i) d -> p i d", i=TILES)
     c_out = out_1.rearrange("(p i) d -> p i d", i=TILES)
+    w_hh_rows = weight_hh.rearrange("(p e) n -> p e n", e=2)
+    a_hh_rows = alpha_weight_hh.rearrange("(p e) n -> p e n", e=2)
 
     with ExitStack() as ctx:
         keep = ctx.enter_context(tc.tile_pool(name="keep", bufs=1))
@@ -49,369 +57,390 @@ def tile_multiinputlstmcell_pa_kernel(
 
         ident = keep.tile([P, P], F32, name="ident")
         ones = keep.tile([P, P], BF16, name="ones")
-        bias_row = keep.tile([P, 4 * H], BF16, name="bias_row")
-        bias_x = keep.tile([P, BANK], F32, name="bias_x")
-        bias_y = keep.tile([P, BANK], F32, name="bias_y")
-        plane_a = keep.tile([P, PASSES, H], U8, name="plane_a", align_bytes=64)
-        plane_w = keep.tile([P, PASSES, 3 * H], U8, name="plane_w", align_bytes=64)
+        bias_row = keep.tile([P, 2 * BANK], BF16, name="bias_row")
+        bias_ai = keep.tile([P, BANK], F32, name="bias_ai")
+        bias_og = keep.tile([P, BANK], F32, name="bias_og")
+        scales_a = keep.tile([P, PASSES, H], U8, name="scales_a", align_bytes=64)
+        scales_w = keep.tile([P, PASSES, 3 * H], U8, name="scales_w", align_bytes=64)
         words_a = keep.tile([P, PASSES, 2 * H], U8, name="words_a", align_bytes=64)
         words_i = keep.tile([P, PASSES, 2 * H], U8, name="words_i", align_bytes=64)
-        words_y = keep.tile([P, PASSES, 2 * BANK], U8, name="words_y", align_bytes=64)
-        w_hh = keep.tile([P, 2, 3 * H], BF16, name="w_hh")
+        words_og = keep.tile([P, PASSES, 2 * BANK], U8, name="words_og", align_bytes=64)
+        w_hh_i = keep.tile([P, 2, H], BF16, name="w_hh_i")
+        w_hh_og = keep.tile([P, 2, BANK], BF16, name="w_hh_og")
         a_hh = keep.tile([P, 2, H], BF16, name="a_hh")
-        h_sb = [keep.tile([P, HEAD, H], BF16, name="h_sb%d" % j) for j in range(2)]
-        c_sb = [keep.tile([P, HEAD, H], BF16, name="c_sb%d" % j) for j in range(2)]
+        h_first = keep.tile([P, 1, H], BF16, name="h_first")
+        h_head = keep.tile([P, STATE_HEAD - 1, H], BF16, name="h_head")
+        h_rest = keep.tile([P, TILES - STATE_HEAD, H], BF16, name="h_rest")
+        c_head = keep.tile([P, STATE_HEAD, H], BF16, name="c_head")
+        c_rest = keep.tile([P, TILES - STATE_HEAD, H], BF16, name="c_rest")
         x_sb = [keep.tile([P, I], BF16, name="x_sb%d" % i) for i in range(TILES)]
 
         make_identity(nc, ident[:])
         nc.vector.memset(bias_row[:], 0.0)
         nc.vector.memset(ones[:], 1.0)
-        for plane in (plane_a, plane_w):
-            nc.vector.memset(plane[:].rearrange("p g n -> p (g n)").bitcast(I32), 0)
+        for scales in (scales_a, scales_w):
+            nc.vector.memset(scales[:].rearrange("p g n -> p (g n)").bitcast(I32), 0)
 
-        def load_scales(queue, plane, scales):
-            for q in range(4):
-                queue.dma_start(
-                    out=plane[32 * q : 32 * q + 4, :, :].bitcast(I32),
-                    in_=scales[:, 4 * q : 4 * q + 4, :].rearrange("g r n -> r g n").bitcast(I32),
+        def load_scales(dst, src):
+            for r in range(4):
+                nc.sync.dma_start(
+                    out=dst[r:P:32, :, :].bitcast(I32),
+                    in_=src[:, r:16:4, :].rearrange("g q n -> q g n").bitcast(I32),
                 )
 
-        def load_words(dst, words):
-            nc.sync.dma_start(out=dst.bitcast(I32), in_=words.rearrange("g p n -> p g n").bitcast(I32))
+        def load_words(dst, src):
+            nc.sync.dma_start(out=dst[:].bitcast(I32), in_=src.rearrange("g p n -> p g n").bitcast(I32))
 
         def load_x(i):
             nc.sync.dma_start(out=x_sb[i][:], in_=x_rows[:, i, :])
 
-        nc.scalar.dma_start(out=bias_row[0:1, H:], in_=bias.rearrange("(o n) -> o n", o=1))
-        nc.scalar.dma_start(out=bias_row[0:1, :H], in_=alpha_bias.rearrange("(o n) -> o n", o=1))
-
-        nc.sync.dma_start(out=h_sb[0][:], in_=h_rows[:, :HEAD, :])
-        nc.sync.dma_start(out=c_sb[0][:], in_=c_rows[:, :HEAD, :])
-        nc.sync.dma_start(out=w_hh[:], in_=weight_hh.rearrange("(p e) n -> p e n", e=2))
-        nc.sync.dma_start(out=a_hh[:], in_=alpha_weight_hh.rearrange("(p e) n -> p e n", e=2))
+        nc.sync.dma_start(out=h_first[:], in_=h_rows[:, :1, :])
+        nc.sync.dma_start(out=w_hh_og[:], in_=w_hh_rows[:, :, H:])
+        nc.sync.dma_start(out=h_head[:], in_=h_rows[:, 1:STATE_HEAD, :])
+        nc.sync.dma_start(out=c_head[:], in_=c_rows[:, :STATE_HEAD, :])
+        nc.sync.dma_start(out=w_hh_i[:], in_=w_hh_rows[:, :, :H])
+        nc.sync.dma_start(out=a_hh[:], in_=a_hh_rows)
+        nc.sync.dma_start(out=bias_row[0:1, H:], in_=bias.rearrange("(o n) -> o n", o=1))
+        nc.sync.dma_start(out=bias_row[0:1, :H], in_=alpha_bias.rearrange("(o n) -> o n", o=1))
         load_x(0)
-        load_scales(nc.sync, plane_a, alpha_weight_ih_scales)
+        load_scales(scales_a, alpha_weight_ih_scales)
         load_x(1)
-        load_scales(nc.sync, plane_w, weight_ih_scales)
-        load_words(words_i[:], weight_ih_words[:, :, : 2 * H])
-        load_words(words_a[:], alpha_weight_ih_words)
-        load_words(words_y[:], weight_ih_words[:, :, 2 * H :])
+        load_scales(scales_w, weight_ih_scales)
+        load_words(words_i, weight_ih_words[:, :, : 2 * H])
+        load_words(words_a, alpha_weight_ih_words)
+        load_words(words_og, weight_ih_words[:, :, 2 * H :])
         load_x(2)
         load_x(3)
-        nc.sync.dma_start(out=h_sb[1][:], in_=h_rows[:, HEAD:, :])
-        nc.sync.dma_start(out=c_sb[1][:], in_=c_rows[:, HEAD:, :])
+        nc.sync.dma_start(out=h_rest[:], in_=h_rows[:, STATE_HEAD:, :])
+        nc.sync.dma_start(out=c_rest[:], in_=c_rows[:, STATE_HEAD:, :])
         for i in range(4, TILES):
             load_x(i)
 
         t = {}
 
-        def transposer(out, in_):
-            return lambda: nc.tensor.transpose(out, in_, ident[:])
+        def bank(tag, shape):
+            return psum.tile(shape, F32, name=tag, bufs=TR_BANKS if tag == "tr" else 1)
 
-        def pairs(words):
+        def pair_buffer(name, i, width=H, count=1):
+            if (name, i // 2) not in t:
+                t[name, i // 2] = work.tile([P, 2, width], F32, name=name, bufs=2)
+            return t[name, i // 2][:, i % 2 : i % 2 + count, :]
+
+        def c_in(i):
+            return (c_head if i < STATE_HEAD else c_rest)[:, i % STATE_HEAD : i % STATE_HEAD + 1, :]
+
+
+        def slots(words):
             view = words.bitcast(BF16).rearrange("p (r e) -> p r e", e=2)
             return [view[:, :, e] for e in range(2)]
 
-        def head_transposes(name, src, tiles, copy):
-            bank = psum.tile([P, len(tiles), P], F32, name="tr", bufs=3)
-            for j, i in enumerate(tiles):
-                nc.tensor.transpose(bank[:, j, :], src[:, i, :].bitcast(F32), ident[:])
-            head_t = keep.tile([P, len(tiles), P], F32, name="%s_head%d" % (name, tiles[0]))
-            copy(out=head_t[:], in_=bank[:])
-            for j, i in enumerate(tiles):
-                t[name + "T", i] = pairs(head_t[:, j, :])
+        def transpose_head_state(name, src, first, copy):
+            count = src.shape[1]
+            ps = bank("tr", [P, count, P])
+            for j in range(count):
+                nc.tensor.transpose(ps[:, j, :], src[:, j, :].bitcast(F32), ident[:])
+            sb = keep.tile([P, count, P], F32, name="%s%d" % (name, first))
+            copy(out=sb[:], in_=ps[:])
+            for j in range(count):
+                t[name, first + j] = slots(sb[:, j, :])
 
-        def plain_banks(i):
-            t["px", i] = psum.tile([P, BANK], F32, name="mx_x" if i == 1 else "plain_x")
-            t["py", i] = psum.tile([P, BANK], F32, name="mx_y" if i == 1 else "plain_y")
+        def spread_bias(dst, cols, tag, copy):
+            ps = bank(tag, [P, BANK])
+            nc.tensor.matmul(ps[:], ones[:], bias_row[:, cols], start=True, stop=True)
+            copy(out=dst[:], in_=ps[:])
 
-        def spread_bias(dst, cols):
-            bank = psum.tile([P, BANK], F32, name="hc")
-            nc.tensor.matmul(bank[:], ones[:], bias_row[:, cols], start=True, stop=True)
-            nc.vector.tensor_copy(out=dst[:], in_=bank[:])
+        def open_plain_banks(i):
+            t["plain_ai", i] = bank({1: "mx_ai", LAST: "tr"}.get(i, "plain_ai"), [P, BANK])
+            t["plain_og", i] = bank({1: "mx_og"}.get(i, "plain_og"), [P, BANK])
 
-        head_transposes("h", h_sb[0], range(HEAD), nc.scalar.copy)
-        spread_bias(bias_x, slice(0, BANK))
-        head_transposes("c", c_sb[0], range(HEAD), nc.scalar.copy)
+        def plain_group(out, state, weights):
+            return [(out, state[e], weights[:, e, :], e == 0, e == 1) for e in range(2)]
 
-        def split_words(i, half):
-            words = x_sb[i][:, I // 2 * half : I // 2 * (half + 1)].bitcast(F32)
-            if (i, half) not in SPLIT:
-                t["xp", i, half] = words.rearrange("p (g m u) -> p g u m", g=2, u=2)
-                return
-            xp = work.tile([P, 2, 2, P], F32, name="xp%d" % half, bufs=2)
-            t["xp", i, half] = xp
-            nc.scalar.copy(out=xp[:], in_=words.rearrange("p (g m u) -> p g u m", g=2, u=2))
+        def plain_og(i):
+            return plain_group(t["plain_og", i][:], t["hT", i], w_hh_og)
 
-        def x_tiles(s):
-            return [i for i in range(TILES) if i - 1 == s]
+        def plain_i(i):
+            return plain_group(t["plain_ai", i][:, GATE_I], t["hT", i], w_hh_i)
 
-        def plain_phase(s, part=None):
-            for i in x_tiles(s):
-                for half in range(2):
-                    if (i, half) not in SPLIT:
-                        split_words(i, half)
-            mats, trs = [], []
-            i = s + 2 if s <= 0 else s
-            if i < 3 and s <= 0 or 3 <= i < TILES:
-                if ("px", i) not in t:
-                    plain_banks(i)
-                px, py = t["px", i], t["py", i]
-                hT = t["hT", i]
-                mats = [
-                    (py[:], hT[0], w_hh[:, 0, H:], i not in EARLY_BIAS, False),
-                    (py[:], hT[1], w_hh[:, 1, H:], False, i not in LATE_BIAS),
-                ]
-                if i in LATE_BIAS:
-                    mats.append((py[:], ones[:], bias_row[:, BANK:], False, True))
-                mats.append((px[:, H:], hT[0], w_hh[:, 0, :H], True, False))
-                mats.append((px[:, H:], hT[1], w_hh[:, 1, :H], False, True))
-                cT = t["cT", i]
-                mats.append((px[:, :H], cT[0], a_hh[:, 0, :], True, False))
-                mats.append((px[:, :H], cT[1], a_hh[:, 1, :], False, True))
-            if part is not None:
-                mats = mats[-4:] if part == "x" else mats[:-4]
-            for i in x_tiles(s):
-                for half in range(2):
-                    bank = psum.tile([P, 2, 2, P], F32, name="tr", bufs=3)
-                    t["xt", i, half] = bank
+        def plain_alpha(i):
+            return plain_group(t["plain_ai", i][:, ALPHA], t["cT", i], a_hh)
+
+        def x_words(i, g, u):
+            if i in PRESORTED and g >= 2:
+                return t["presorted", i][:, g - 2, u, :]
+            return x_sb[i][:].bitcast(F32)[:, 2 * P * g + u : 2 * P * (g + 1) : 2]
+
+        def x_transposes(i):
+            jobs = []
+            for half in range(2):
+                t["xT", i, half] = bank("tr", [P, 2, 2, P])
+                for u in range(2):
                     for g in range(2):
-                        for u in range(2):
-                            trs.append(transposer(bank[:, g, u, :], t["xp", i, half][:, g, u, :]))
-            i = s + 1
-            if HEAD <= i < TILES and i % 2 == 0:
-                bank = psum.tile([P, 2, 2, P], F32, name="hc")
-                t["hc", i] = bank
-                for j in range(2):
-                    trs.append(transposer(bank[:, j, 0, :], h_sb[1][:, i + j - HEAD, :].bitcast(F32)))
-                    trs.append(transposer(bank[:, j, 1, :], c_sb[1][:, i + j - HEAD, :].bitcast(F32)))
-            gaps = max(len(mats) - 1, 1)
-            share = [len(trs) // gaps + (j < len(trs) % gaps) for j in range(gaps)] + [0]
-            for (out, lhs, rhs, start, stop), n in zip(mats, share):
-                nc.tensor.matmul(out, lhs, rhs, start=start, stop=stop)
-                for tr in trs[:n]:
-                    tr()
-                trs = trs[n:]
-            for tr in trs:
-                tr()
-            if s == -2:
-                spread_bias(bias_y, slice(BANK, 2 * BANK))
+                        jobs.append((t["xT", i, half][:, g, u, :], x_words(i, 2 * half + g, u)))
+            return jobs
 
-        def mx_group(i, out, words, plane, col0, ncols, wcol0):
-            codes, scales = t["codes", i], t["scales", i]
+        def state_transposes(i):
+            t["stateT", i] = bank("state", [P, 2, 2, P])
+            return [
+                (t["stateT", i][:, j, n, :], src[:, i + j - STATE_HEAD, :].bitcast(F32))
+                for j in range(2)
+                for n, src in enumerate((h_rest, c_rest))
+            ]
+
+        def weave(matmuls, transposes=(), gaps=1):
+            done = 0
+            for j, (out, lhsT, rhs, start, stop) in enumerate(matmuls):
+                nc.tensor.matmul(out, lhsT, rhs, start=start, stop=stop)
+                upto = min(done + len(transposes) // gaps + (j < len(transposes) % gaps), len(transposes))
+                for out_t, in_t in transposes[done:upto]:
+                    nc.tensor.transpose(out_t, in_t, ident[:])
+                done = upto
+            for out_t, in_t in transposes[done:]:
+                nc.tensor.transpose(out_t, in_t, ident[:])
+
+        def mx_group(i, out, words, scales):
             for g in range(PASSES):
                 nc.tensor.matmul_mx(
                     out=out,
-                    lhsT=codes[:, P * g : P * (g + 1)].bitcast(E5M2X4),
-                    lhsT_scale=scales[:, P * g : P * (g + 1)],
-                    rhs=words[:, g, 2 * wcol0 : 2 * (wcol0 + ncols)].bitcast(E2M1X4),
-                    rhs_scale=plane[:, g, col0 : col0 + ncols],
+                    lhsT=t["x_codes", i][:, P * g : P * (g + 1)].bitcast(E5M2X4),
+                    lhsT_scale=t["x_scales", i][:, P * g : P * (g + 1)],
+                    rhs=words[:, g, :].bitcast(E2M1X4),
+                    rhs_scale=scales[:, g, :],
                     start=(g == 0),
                     stop=(g == PASSES - 1),
                 )
 
-        def mx_x(i):
-            bank = psum.tile([P, BANK], F32, name="mx_x")
-            t["mx", i] = bank
-            mx_group(i, bank[:, H:], words_i, plane_w, 0, H, 0)
-            mx_group(i, bank[:, :H], words_a, plane_a, 0, H, 0)
+        def mx_operands(name, cols):
+            if name == "og":
+                return words_og[:, :, 2 * cols.start : 2 * cols.stop], scales_w[:, :, H + cols.start : H + cols.stop]
+            return (words_a[:], scales_a[:]) if cols == ALPHA else (words_i[:], scales_w[:, :, :H])
 
-        def mx_y(i):
-            bank = psum.tile([P, BANK], F32, name="mx_y")
-            t["my", i] = bank
-            mx_group(i, bank[:], words_y, plane_w, H, BANK, 0)
+        def mx_ai(i):
+            t["mx_ai", i, 0] = bank("mx_ai", [P, BANK])
+            for cols in (GATE_I, ALPHA):
+                mx_group(i, t["mx_ai", i, 0][:, cols], *mx_operands("ai", cols))
 
-        def mx_x_part(i, cols, words, plane, tag, bufs):
-            bank = psum.tile([P, H], F32, name=tag, bufs=bufs)
-            t["mx", i, cols] = bank
-            mx_group(i, bank[:], words, plane, 0, H, 0)
+        def mx_og(i):
+            t["mx_og", i, 0] = bank("mx_og", [P, BANK])
+            mx_group(i, t["mx_og", i, 0][:], *mx_operands("og", WHOLE))
 
-        def pre_x_part(i, cols):
-            nc.vector.tensor_tensor(
-                out=buf("pre_x", i, 1, BANK)[:, 0, cols : cols + H],
-                in0=t["mx", i, cols][:],
-                in1=t["rec_x", i][:, cols : cols + H],
-                op=ALU.add,
-            )
+        def mx_gate(name, i, cols, tag):
+            t["mx_" + name, i, cols.start] = bank(tag, [P, H])
+            mx_group(i, t["mx_" + name, i, cols.start][:], *mx_operands(name, cols))
 
-        def gates_x_part(i, cols):
-            nc.scalar.activation(
-                out=buf("gate_x", i, 1, BANK)[:, 0, cols : cols + H],
-                in_=buf("pre_x", i, 1, BANK)[:, 0, cols : cols + H],
-                func=ACT.Sigmoid,
-            )
 
-        def mx_y_part(i, cols, tag, bufs):
-            bank = psum.tile([P, H], F32, name=tag, bufs=bufs)
-            t["my", i, cols] = bank
-            mx_group(i, bank[:], words_y, plane_w, H + cols, H, cols)
+        def presort(i):
+            if i in PRESORTED:
+                t["presorted", i] = work.tile([P, 2, 2, P], F32, name="presorted", bufs=2)
+                words = x_sb[i][:, I // 2 :].bitcast(F32)
+                nc.scalar.copy(out=t["presorted", i][:], in_=words.rearrange("p (g m u) -> p g u m", g=2, u=2))
 
-        def pre_y_part(i, cols):
-            nc.vector.tensor_tensor(
-                out=buf("pre_y", i, 1, BANK)[:, 0, cols : cols + H],
-                in0=t["my", i, cols][:],
-                in1=t["rec_y", i][:, cols : cols + H],
-                op=ALU.add,
-            )
-
-        def copy_xt(i, half):
+        def copy_xT(i, half):
             if half == 0:
-                t["grouped", i] = work.tile([P, 2, 2, P, 2], F32, name="grouped", bufs=3, align_bytes=64)
-            copy = nc.vector.tensor_copy if half == 0 and i in V_COPY else nc.scalar.copy
-            copy(out=t["grouped", i][:, half], in_=t["xt", i, half][:].rearrange("p g u r -> p g r u"))
+                t["grouped", i] = work.tile([P, 2, 2, P, 2], F32, name="grouped", align_bytes=64)
+            copy = nc.vector.tensor_copy if half == 0 and i in FIRST_BANK_ON_VECTOR else nc.scalar.copy
+            copy(out=t["grouped", i][:, half], in_=t["xT", i, half][:].rearrange("p g u r -> p g r u"))
 
-        def quant(i):
-            codes = work.tile([P, PASSES * P], U32, name="codes", align_bytes=64)
-            scales = work.tile([P, PASSES * P], U8, name="scales", align_bytes=64)
-            t["codes", i], t["scales", i] = codes, scales
+        def quantize(i):
+            t["x_codes", i] = work.tile([P, PASSES * P], U32, name="x_codes", align_bytes=64)
+            t["x_scales", i] = work.tile([P, PASSES * P], U8, name="x_scales", align_bytes=64)
             nc.vector.quantize_mx(
-                out=codes[:].bitcast(E5M2X4),
-                scales=scales[:],
+                out=t["x_codes", i][:].bitcast(E5M2X4),
+                scales=t["x_scales", i][:],
                 in_=t["grouped", i][:].rearrange("p a g r u -> p (a g r u)").bitcast(BF16),
             )
 
-        def copy_hc(i):
-            hc = work.tile([P, 2, 2, P], F32, name="hc_sb", bufs=2)
-            nc.scalar.copy(out=hc[:], in_=t["hc", i][:])
+        def copy_stateT(i):
+            sb = work.tile([P, 2, 2, P], F32, name="stateT_sb", bufs=2)
+            nc.scalar.copy(out=sb[:], in_=t["stateT", i][:])
             for j in range(2):
-                t["hT", i + j], t["cT", i + j] = pairs(hc[:, j, 0, :]), pairs(hc[:, j, 1, :])
+                t["hT", i + j], t["cT", i + j] = slots(sb[:, j, 0, :]), slots(sb[:, j, 1, :])
 
-        def new(name, i, width, bufs=3):
-            t[name, i] = work.tile([P, width], F32, name=name, bufs=bufs)
-            return t[name, i]
+        def add_bias(i, name):
+            t["biased_" + name, i] = work.tile([P, BANK], F32, name="biased_" + name, bufs=PLAIN_HEAD + 1)
+            nc.vector.tensor_tensor(
+                out=t["biased_" + name, i][:],
+                in0=t["plain_" + name, i][:],
+                in1=(bias_ai if name == "ai" else bias_og)[:],
+                op=ALU.add,
+            )
 
-        def plain_x_out(i):
-            nc.vector.tensor_tensor(out=new("rec_x", i, BANK, 4)[:], in0=t["px", i][:], in1=bias_x[:], op=ALU.add)
 
-        def plain_y_out(i):
-            if i in EARLY_BIAS or i in LATE_BIAS:
-                nc.scalar.copy(out=new("rec_y", i, BANK, 4)[:], in_=t["py", i][:])
+        def add_mx(i, name, cols=WHOLE):
+            nc.vector.tensor_tensor(
+                out=pair_buffer("pre_" + name, i, BANK)[:, 0, cols],
+                in0=t["mx_" + name, i, cols.start][:],
+                in1=t["biased_" + name, i][:, cols],
+                op=ALU.add,
+            )
+
+        def gates_ai(i, cols=WHOLE):
+            nc.scalar.activation(
+                out=pair_buffer("gates_ai", i, BANK)[:, 0, cols],
+                in_=pair_buffer("pre_ai", i, BANK)[:, 0, cols],
+                func=ACT.Sigmoid,
+            )
+
+        def gate_g(i):
+            nc.scalar.activation(out=pair_buffer("g", i), in_=pair_buffer("pre_og", i, BANK)[:, :, GATE_G], func=ACT.Tanh)
+
+        def gate_o(i):
+            nc.scalar.activation(out=pair_buffer("o", i), in_=pair_buffer("pre_og", i, BANK)[:, :, GATE_O], func=ACT.Sigmoid)
+
+        def diff(i):
+            gates = pair_buffer("gates_ai", i, BANK)
+            engine = nc.gpsimd if i in DIFF_ON_GPSIMD else nc.vector
+            engine.tensor_tensor(out=pair_buffer("diff", i), in0=gates[:, :, GATE_I], in1=gates[:, :, ALPHA], op=ALU.subtract)
+
+        def weight(i):
+            nc.scalar.activation(out=pair_buffer("w", i), in_=pair_buffer("diff", i), func=ACT.Sigmoid)
+
+        def cell_term(i):
+            if i in CELL_ON_GPSIMD:
+                nc.gpsimd.tensor_tensor(out=pair_buffer("term", i), in0=pair_buffer("g", i), in1=c_in(i), op=ALU.subtract)
             else:
-                nc.vector.tensor_tensor(out=new("rec_y", i, BANK, 4)[:], in0=t["py", i][:], in1=bias_y[:], op=ALU.add)
+                nc.vector.scalar_tensor_tensor(
+                    out=pair_buffer("term", i), in0=pair_buffer("w", i), scalar=-1.0, in1=c_in(i), op0=ALU.add, op1=ALU.mult
+                )
 
-        def eng(name, i):
-            return nc.gpsimd if i in G_TILES[name] else nc.vector
+        def cell_product(i):
+            engine, factor = (nc.gpsimd, "term") if i in CELL_ON_GPSIMD else (nc.vector, "g")
+            engine.tensor_tensor(
+                out=pair_buffer("product", i), in0=pair_buffer("w", i), in1=pair_buffer(factor, i), op=ALU.mult
+            )
 
-        def buf(name, i, n, width=H):
-            key = name, i // 2
-            if key not in t:
-                t[key] = work.tile([P, 2, width], F32, name=name, bufs=2)
-            return t[key][:, i % 2 : i % 2 + n, :]
+        def cell(i):
+            if i in CELL_ON_GPSIMD:
+                nc.gpsimd.tensor_tensor(out=pair_buffer("c_1", i), in0=pair_buffer("product", i), in1=c_in(i), op=ALU.add)
+            else:
+                nc.vector.tensor_tensor(
+                    out=pair_buffer("c_1", i), in0=pair_buffer("product", i), in1=pair_buffer("term", i), op=ALU.subtract
+                )
+            nc.sync.dma_start(out=c_out[:, i : i + 1, :], in_=pair_buffer("c_1", i))
 
-        def pre_x(i):
-            nc.vector.tensor_tensor(out=buf("pre_x", i, 1, BANK)[:, 0, :], in0=t["mx", i][:], in1=t["rec_x", i][:], op=ALU.add)
+        def tanh_cell(i):
+            nc.scalar.activation(out=pair_buffer("tanh_c", i), in_=pair_buffer("c_1", i), func=ACT.Tanh)
 
-        def pre_y(i):
-            nc.vector.tensor_tensor(out=buf("pre_y", i, 1, BANK)[:, 0, :], in0=t["my", i][:], in1=t["rec_y", i][:], op=ALU.add)
-
-        def gates_x(i, n):
-            nc.scalar.activation(out=buf("gate_x", i, n, BANK), in_=buf("pre_x", i, n, BANK), func=ACT.Sigmoid)
-
-        def gate_g(i, n):
-            nc.scalar.activation(out=buf("g", i, n), in_=buf("pre_y", i, n, BANK)[:, :, H:], func=ACT.Tanh)
-
-        def gate_o(i, n):
-            nc.scalar.activation(out=buf("o", i, n), in_=buf("pre_y", i, n, BANK)[:, :, :H], func=ACT.Sigmoid)
-
-        def diff(i, n):
-            gx = buf("gate_x", i, n, BANK)
-            eng("d", i).tensor_tensor(out=buf("d", i, n), in0=gx[:, :, H:], in1=gx[:, :, :H], op=ALU.subtract)
-
-        def weight(i, n):
-            nc.scalar.activation(out=buf("w", i, n), in_=buf("d", i, n), func=ACT.Sigmoid)
-
-        def c_in(i, n):
-            return c_sb[i // HEAD][:, i % HEAD : i % HEAD + n, :]
-
-        def keep_c(i, n):
-            eng("u", i).tensor_tensor(out=buf("u", i, n), in0=buf("g", i, n), in1=c_in(i, n), op=ALU.subtract)
-
-        def take_g(i, n):
-            eng("m", i).tensor_tensor(out=buf("m", i, n), in0=buf("w", i, n), in1=buf("u", i, n), op=ALU.mult)
-
-        def cell(i, n):
-            eng("c1", i).tensor_tensor(out=buf("c1", i, n), in0=buf("m", i, n), in1=c_in(i, n), op=ALU.add)
-            nc.sync.dma_start(out=c_out[:, i : i + n, :], in_=buf("c1", i, n))
-
-        def tanh_cell(i, n):
-            nc.scalar.activation(out=buf("tc", i, n), in_=buf("c1", i, n), func=ACT.Tanh)
-
-        def hidden(i, n):
-            eng("h1", i).tensor_tensor(out=buf("h1", i, n), in0=buf("o", i, n), in1=buf("tc", i, n), op=ALU.mult)
-            nc.sync.dma_start(out=h_out[:, i : i + n, :], in_=buf("h1", i, n))
-
-        def split(i):
-            for half in range(2):
-                if (i, half) in SPLIT:
-                    split_words(i, half)
-
-        def plain_tile(s):
-            return s + 2 if s <= 0 else (s if s >= 3 else -1)
+        def hidden(i, count=1, engine=nc.vector):
+            engine.tensor_tensor(
+                out=pair_buffer("h_1", i, count=count),
+                in0=pair_buffer("o", i, count=count),
+                in1=pair_buffer("tanh_c", i, count=count),
+                op=ALU.mult,
+            )
+            nc.sync.dma_start(out=h_out[:, i : i + count, :], in_=pair_buffer("h_1", i, count=count))
 
         def run(fn, i, *args):
             if 0 <= i < TILES:
                 fn(i, *args)
 
-        for s in range(-2, 7):
-            plain_phase(s)
-            run(pre_y, s - 1)
-            run(gates_x, s - 1, 1)
-            run(cell, s - 2, 1)
-            run(copy_xt, s + 1, 0)
-            run(gate_g, s - 1, 1)
-            run(diff, s - 1, 1)
-            run(copy_xt, s + 1, 1)
-            run(keep_c, s - 1, 1)
-            run(plain_y_out, plain_tile(s))
-            if s < 0: run(quant, s + 1)
-            run(plain_x_out, plain_tile(s))
-            run(weight, s - 1, 1)
-            if s >= 0: run(quant, s + 1)
-            if ("hc", s + 1) in t: copy_hc(s + 1)
-            run(tanh_cell, s - 2, 1)
-            run(take_g, s - 1, 1)
-            run(split, s + 2)
-            run(gate_o, s - 1, 1)
-            run(mx_x, s + 0)
-            run(mx_y, s + 0)
-            run(pre_x, s + 0)
-            if s % 2 == 1: run(hidden, s - 3, 2)
+        transpose_head_state("hT", h_first, 0, nc.scalar.copy)
+        open_plain_banks(0)
+        weave(plain_og(0))
+        transpose_head_state("hT", h_head, 1, nc.vector.tensor_copy)
+        transpose_head_state("cT", c_head, 0, nc.scalar.copy)
+        weave(plain_i(0))
+        spread_bias(bias_og, slice(BANK, 2 * BANK), "state", nc.vector.tensor_copy)
+        spread_bias(bias_ai, WHOLE, "tr", nc.scalar.copy)
+        weave(plain_alpha(0))
+        add_bias(0, "og")
+        add_bias(0, "ai")
 
-        hidden(4, 1)
-        plain_phase(7, "x")
-        gates_x(6, 1)
-        pre_y(6)
-        cell(5, 1)
-        plain_x_out(7)
-        gate_g(6, 1)
-        diff(6, 1)
-        keep_c(6, 1)
-        mx_x_part(7, H, words_i, plane_w, "mx_x", 1)
-        mx_x_part(7, 0, words_a, plane_a, "hc", 1)
-        plain_phase(7, "y")
-        mx_y_part(7, H, "mx_y", 1)
-        mx_y_part(7, 0, "tr", 3)
-        pre_x_part(7, H)
-        weight(6, 1)
-        gates_x_part(7, H)
-        pre_x_part(7, 0)
-        gates_x_part(7, 0)
-        take_g(6, 1)
-        plain_y_out(7)
-        tanh_cell(5, 1)
-        diff(7, 1)
-        pre_y_part(7, H)
-        weight(7, 1)
-        gate_g(7, 1)
-        cell(6, 1)
-        hidden(5, 1)
-        keep_c(7, 1)
-        gate_o(6, 1)
-        tanh_cell(6, 1)
-        pre_y_part(7, 0)
-        take_g(7, 1)
-        gate_o(7, 1)
-        cell(7, 1)
-        hidden(6, 1)
-        tanh_cell(7, 1)
-        hidden(7, 1)
+        def plain_tile(s):
+            if s + 2 < PLAIN_HEAD:
+                return s + 2
+            return s if s >= PLAIN_HEAD else -1
+
+        def plain_and_transposes(s, gaps):
+            i = plain_tile(s)
+            matmuls = []
+            if i >= 0:
+                open_plain_banks(i)
+                matmuls = plain_og(i) + plain_i(i) + plain_alpha(i)
+            transposes = x_transposes(s + 1)
+            if s + 1 >= STATE_HEAD and s % 2 == 1:
+                transposes = transposes + state_transposes(s + 1)
+            weave(matmuls, transposes, gaps)
+
+        for s in range(-1, LAST - 1):
+            plain_and_transposes(s, gaps=5)
+            run(add_mx, s - 1, "og")
+            run(gates_ai, s - 1)
+            run(cell, s - 2)
+            copy_xT(s + 1, 0)
+            run(gate_g, s - 1)
+            run(diff, s - 1)
+            copy_xT(s + 1, 1)
+            run(cell_term, s - 1)
+            run(add_bias, plain_tile(s), "og")
+            run(add_bias, plain_tile(s), "ai")
+            run(weight, s - 1)
+            quantize(s + 1)
+            if ("stateT", s + 1) in t:
+                copy_stateT(s + 1)
+            run(tanh_cell, s - 2)
+            run(cell_product, s - 1)
+            presort(s + 2)
+            run(gate_o, s - 1)
+            run(mx_ai, s)
+            run(mx_og, s)
+            run(add_mx, s, "ai")
+            if s % 2 == 1:
+                run(hidden, s - 3, 2)
+
+        w, x, y, z = LAST - 3, LAST - 2, LAST - 1, LAST
+        plain_and_transposes(y, gaps=3)
+        add_mx(x, "og")
+        gates_ai(x)
+        cell(w)
+        copy_xT(z, 0)
+        copy_xT(z, 1)
+        gate_g(x)
+        diff(x)
+        cell_term(x)
+        add_bias(y, "og")
+        quantize(z)
+        add_bias(y, "ai")
+        weight(x)
+        tanh_cell(w)
+        cell_product(x)
+        hidden(w, engine=nc.gpsimd)
+        gate_o(x)
+
+        mx_ai(y)
+        open_plain_banks(z)
+        weave(plain_i(z) + plain_alpha(z))
+        mx_gate("ai", z, GATE_I, "state")
+        mx_gate("ai", z, ALPHA, "tr")
+        add_mx(y, "ai")
+        add_bias(z, "ai")
+        weave(plain_og(z))
+        mx_gate("og", y, GATE_G, "mx_og")
+        mx_gate("og", z, GATE_G, "tr")
+        mx_gate("og", y, GATE_O, "mx_ai")
+        mx_gate("og", z, GATE_O, "plain_ai")
+
+        gates_ai(y)
+        cell(x)
+        for cols in (GATE_I, ALPHA):
+            add_mx(z, "ai", cols)
+            gates_ai(z, cols)
+        diff(y)
+        tanh_cell(x)
+        weight(y)
+        add_bias(z, "og")
+        diff(z)
+        add_mx(y, "og", GATE_G)
+        gate_g(y)
+        add_mx(z, "og", GATE_G)
+        weight(z)
+        gate_g(z)
+        for i in (y, z):
+            cell_term(i)
+            cell_product(i)
+            add_mx(i, "og", GATE_O)
+            cell(i)
+            gate_o(i)
+            tanh_cell(i)
+        for i in (x, y, z):
+            hidden(i)

from contextlib import ExitStack

import concourse.mybir as mybir
from concourse.masks import make_identity

B, I, H = 1024, 2048, 256
FLOPS = 2 * B * I * 4 * H + 2 * B * H * 4 * H

F32 = mybir.dt.float32
BF16 = mybir.dt.bfloat16
I32 = mybir.dt.int32
U32 = mybir.dt.uint32
U8 = mybir.dt.uint8
E5M2X4 = mybir.dt.float8_e5m2_x4
E2M1X4 = mybir.dt.float4_e2m1fn_x4
ACT = mybir.ActivationFunctionType
ALU = mybir.AluOpType

P = 128
TILES = B // P
LAST = TILES - 1
PASSES = I // (4 * P)
BANK = 2 * H
ALPHA, GATE_I = slice(0, H), slice(H, BANK)
GATE_O, GATE_G = slice(0, H), slice(H, BANK)
WHOLE = slice(0, BANK)

STATE_HEAD = TILES // 2
PLAIN_HEAD = 3
TR_BANKS = 3

PRESORTED = range(PLAIN_HEAD, TILES)
FIRST_BANK_ON_VECTOR = range(2, LAST)
DIFF_ON_GPSIMD = range(2, TILES)
CELL_ON_GPSIMD = range(LAST - 1)


def tile_multiinputlstmcell_pa_kernel(
    tc, input_, c_input, h_0, weight_ih_words, weight_ih_scales, weight_hh,
    alpha_weight_ih_words, alpha_weight_ih_scales, alpha_weight_hh, bias, alpha_bias,
    out_0, out_1,
):
    nc = tc.nc
    x_rows = input_.rearrange("(p i) k -> p i k", i=TILES)
    h_rows = h_0.rearrange("(p i) d -> p i d", i=TILES)
    c_rows = c_input.rearrange("(p i) o d -> p i (o d)", i=TILES)
    h_out = out_0.rearrange("(p i) d -> p i d", i=TILES)
    c_out = out_1.rearrange("(p i) d -> p i d", i=TILES)
    w_hh_rows = weight_hh.rearrange("(p e) n -> p e n", e=2)
    a_hh_rows = alpha_weight_hh.rearrange("(p e) n -> p e n", e=2)

    with ExitStack() as ctx:
        keep = ctx.enter_context(tc.tile_pool(name="keep", bufs=1))
        work = ctx.enter_context(tc.tile_pool(name="work", bufs=3))
        psum = ctx.enter_context(tc.psum_pool(name="psum", bufs=1))
        ctx.enter_context(tc.manual_schedule())

        ident = keep.tile([P, P], F32, name="ident")
        ones = keep.tile([P, P], BF16, name="ones")
        bias_row = keep.tile([P, 2 * BANK], BF16, name="bias_row")
        bias_ai = keep.tile([P, BANK], F32, name="bias_ai")
        bias_og = keep.tile([P, BANK], F32, name="bias_og")
        scales_a = keep.tile([P, PASSES, H], U8, name="scales_a", align_bytes=64)
        scales_w = keep.tile([P, PASSES, 3 * H], U8, name="scales_w", align_bytes=64)
        words_a = keep.tile([P, PASSES, 2 * H], U8, name="words_a", align_bytes=64)
        words_i = keep.tile([P, PASSES, 2 * H], U8, name="words_i", align_bytes=64)
        words_og = keep.tile([P, PASSES, 2 * BANK], U8, name="words_og", align_bytes=64)
        w_hh_i = keep.tile([P, 2, H], BF16, name="w_hh_i")
        w_hh_og = keep.tile([P, 2, BANK], BF16, name="w_hh_og")
        a_hh = keep.tile([P, 2, H], BF16, name="a_hh")
        h_first = keep.tile([P, 1, H], BF16, name="h_first")
        h_head = keep.tile([P, STATE_HEAD - 1, H], BF16, name="h_head")
        h_rest = keep.tile([P, TILES - STATE_HEAD, H], BF16, name="h_rest")
        c_head = keep.tile([P, STATE_HEAD, H], BF16, name="c_head")
        c_rest = keep.tile([P, TILES - STATE_HEAD, H], BF16, name="c_rest")
        x_sb = [keep.tile([P, I], BF16, name="x_sb%d" % i) for i in range(TILES)]

        make_identity(nc, ident[:])
        nc.vector.memset(bias_row[:], 0.0)
        nc.vector.memset(ones[:], 1.0)
        for scales in (scales_a, scales_w):
            nc.vector.memset(scales[:].rearrange("p g n -> p (g n)").bitcast(I32), 0)

        def load_scales(dst, src):
            for r in range(4):
                nc.sync.dma_start(
                    out=dst[r:P:32, :, :].bitcast(I32),
                    in_=src[:, r:16:4, :].rearrange("g q n -> q g n").bitcast(I32),
                )

        def load_words(dst, src):
            nc.sync.dma_start(out=dst[:].bitcast(I32), in_=src.rearrange("g p n -> p g n").bitcast(I32))

        def load_x(i):
            nc.sync.dma_start(out=x_sb[i][:], in_=x_rows[:, i, :])

        nc.sync.dma_start(out=h_first[:], in_=h_rows[:, :1, :])
        nc.sync.dma_start(out=w_hh_og[:], in_=w_hh_rows[:, :, H:])
        nc.sync.dma_start(out=h_head[:], in_=h_rows[:, 1:STATE_HEAD, :])
        nc.sync.dma_start(out=c_head[:], in_=c_rows[:, :STATE_HEAD, :])
        nc.sync.dma_start(out=w_hh_i[:], in_=w_hh_rows[:, :, :H])
        nc.sync.dma_start(out=a_hh[:], in_=a_hh_rows)
        nc.sync.dma_start(out=bias_row[0:1, H:], in_=bias.rearrange("(o n) -> o n", o=1))
        nc.sync.dma_start(out=bias_row[0:1, :H], in_=alpha_bias.rearrange("(o n) -> o n", o=1))
        load_x(0)
        load_scales(scales_a, alpha_weight_ih_scales)
        load_x(1)
        load_scales(scales_w, weight_ih_scales)
        load_words(words_i, weight_ih_words[:, :, : 2 * H])
        load_words(words_a, alpha_weight_ih_words)
        load_words(words_og, weight_ih_words[:, :, 2 * H :])
        load_x(2)
        load_x(3)
        nc.sync.dma_start(out=h_rest[:], in_=h_rows[:, STATE_HEAD:, :])
        nc.sync.dma_start(out=c_rest[:], in_=c_rows[:, STATE_HEAD:, :])
        for i in range(4, TILES):
            load_x(i)

        t = {}

        def bank(tag, shape):
            return psum.tile(shape, F32, name=tag, bufs=TR_BANKS if tag == "tr" else 1)

        def pair_buffer(name, i, width=H, count=1):
            if (name, i // 2) not in t:
                t[name, i // 2] = work.tile([P, 2, width], F32, name=name, bufs=2)
            return t[name, i // 2][:, i % 2 : i % 2 + count, :]

        def c_in(i):
            return (c_head if i < STATE_HEAD else c_rest)[:, i % STATE_HEAD : i % STATE_HEAD + 1, :]


        def slots(words):
            view = words.bitcast(BF16).rearrange("p (r e) -> p r e", e=2)
            return [view[:, :, e] for e in range(2)]

        def transpose_head_state(name, src, first, copy):
            count = src.shape[1]
            ps = bank("tr", [P, count, P])
            for j in range(count):
                nc.tensor.transpose(ps[:, j, :], src[:, j, :].bitcast(F32), ident[:])
            sb = keep.tile([P, count, P], F32, name="%s%d" % (name, first))
            copy(out=sb[:], in_=ps[:])
            for j in range(count):
                t[name, first + j] = slots(sb[:, j, :])

        def spread_bias(dst, cols, tag, copy):
            ps = bank(tag, [P, BANK])
            nc.tensor.matmul(ps[:], ones[:], bias_row[:, cols], start=True, stop=True)
            copy(out=dst[:], in_=ps[:])

        def open_plain_banks(i):
            t["plain_ai", i] = bank({1: "mx_ai", LAST: "tr"}.get(i, "plain_ai"), [P, BANK])
            t["plain_og", i] = bank({1: "mx_og"}.get(i, "plain_og"), [P, BANK])

        def plain_group(out, state, weights):
            return [(out, state[e], weights[:, e, :], e == 0, e == 1) for e in range(2)]

        def plain_og(i):
            return plain_group(t["plain_og", i][:], t["hT", i], w_hh_og)

        def plain_i(i):
            return plain_group(t["plain_ai", i][:, GATE_I], t["hT", i], w_hh_i)

        def plain_alpha(i):
            return plain_group(t["plain_ai", i][:, ALPHA], t["cT", i], a_hh)

        def x_words(i, g, u):
            if i in PRESORTED and g >= 2:
                return t["presorted", i][:, g - 2, u, :]
            return x_sb[i][:].bitcast(F32)[:, 2 * P * g + u : 2 * P * (g + 1) : 2]

        def x_transposes(i):
            jobs = []
            for half in range(2):
                t["xT", i, half] = bank("tr", [P, 2, 2, P])
                for u in range(2):
                    for g in range(2):
                        jobs.append((t["xT", i, half][:, g, u, :], x_words(i, 2 * half + g, u)))
            return jobs

        def state_transposes(i):
            t["stateT", i] = bank("state", [P, 2, 2, P])
            return [
                (t["stateT", i][:, j, n, :], src[:, i + j - STATE_HEAD, :].bitcast(F32))
                for j in range(2)
                for n, src in enumerate((h_rest, c_rest))
            ]

        def weave(matmuls, transposes=(), gaps=1):
            done = 0
            for j, (out, lhsT, rhs, start, stop) in enumerate(matmuls):
                nc.tensor.matmul(out, lhsT, rhs, start=start, stop=stop)
                upto = min(done + len(transposes) // gaps + (j < len(transposes) % gaps), len(transposes))
                for out_t, in_t in transposes[done:upto]:
                    nc.tensor.transpose(out_t, in_t, ident[:])
                done = upto
            for out_t, in_t in transposes[done:]:
                nc.tensor.transpose(out_t, in_t, ident[:])

        def mx_group(i, out, words, scales):
            for g in range(PASSES):
                nc.tensor.matmul_mx(
                    out=out,
                    lhsT=t["x_codes", i][:, P * g : P * (g + 1)].bitcast(E5M2X4),
                    lhsT_scale=t["x_scales", i][:, P * g : P * (g + 1)],
                    rhs=words[:, g, :].bitcast(E2M1X4),
                    rhs_scale=scales[:, g, :],
                    start=(g == 0),
                    stop=(g == PASSES - 1),
                )

        def mx_operands(name, cols):
            if name == "og":
                return words_og[:, :, 2 * cols.start : 2 * cols.stop], scales_w[:, :, H + cols.start : H + cols.stop]
            return (words_a[:], scales_a[:]) if cols == ALPHA else (words_i[:], scales_w[:, :, :H])

        def mx_ai(i):
            t["mx_ai", i, 0] = bank("mx_ai", [P, BANK])
            for cols in (GATE_I, ALPHA):
                mx_group(i, t["mx_ai", i, 0][:, cols], *mx_operands("ai", cols))

        def mx_og(i):
            t["mx_og", i, 0] = bank("mx_og", [P, BANK])
            mx_group(i, t["mx_og", i, 0][:], *mx_operands("og", WHOLE))

        def mx_gate(name, i, cols, tag):
            t["mx_" + name, i, cols.start] = bank(tag, [P, H])
            mx_group(i, t["mx_" + name, i, cols.start][:], *mx_operands(name, cols))


        def presort(i):
            if i in PRESORTED:
                t["presorted", i] = work.tile([P, 2, 2, P], F32, name="presorted", bufs=2)
                words = x_sb[i][:, I // 2 :].bitcast(F32)
                nc.scalar.copy(out=t["presorted", i][:], in_=words.rearrange("p (g m u) -> p g u m", g=2, u=2))

        def copy_xT(i, half):
            if half == 0:
                t["grouped", i] = work.tile([P, 2, 2, P, 2], F32, name="grouped", align_bytes=64)
            copy = nc.vector.tensor_copy if half == 0 and i in FIRST_BANK_ON_VECTOR else nc.scalar.copy
            copy(out=t["grouped", i][:, half], in_=t["xT", i, half][:].rearrange("p g u r -> p g r u"))

        def quantize(i):
            t["x_codes", i] = work.tile([P, PASSES * P], U32, name="x_codes", align_bytes=64)
            t["x_scales", i] = work.tile([P, PASSES * P], U8, name="x_scales", align_bytes=64)
            nc.vector.quantize_mx(
                out=t["x_codes", i][:].bitcast(E5M2X4),
                scales=t["x_scales", i][:],
                in_=t["grouped", i][:].rearrange("p a g r u -> p (a g r u)").bitcast(BF16),
            )

        def copy_stateT(i):
            sb = work.tile([P, 2, 2, P], F32, name="stateT_sb", bufs=2)
            nc.scalar.copy(out=sb[:], in_=t["stateT", i][:])
            for j in range(2):
                t["hT", i + j], t["cT", i + j] = slots(sb[:, j, 0, :]), slots(sb[:, j, 1, :])

        def add_bias(i, name):
            t["biased_" + name, i] = work.tile([P, BANK], F32, name="biased_" + name, bufs=PLAIN_HEAD + 1)
            nc.vector.tensor_tensor(
                out=t["biased_" + name, i][:],
                in0=t["plain_" + name, i][:],
                in1=(bias_ai if name == "ai" else bias_og)[:],
                op=ALU.add,
            )


        def add_mx(i, name, cols=WHOLE):
            nc.vector.tensor_tensor(
                out=pair_buffer("pre_" + name, i, BANK)[:, 0, cols],
                in0=t["mx_" + name, i, cols.start][:],
                in1=t["biased_" + name, i][:, cols],
                op=ALU.add,
            )

        def gates_ai(i, cols=WHOLE):
            nc.scalar.activation(
                out=pair_buffer("gates_ai", i, BANK)[:, 0, cols],
                in_=pair_buffer("pre_ai", i, BANK)[:, 0, cols],
                func=ACT.Sigmoid,
            )

        def gate_g(i):
            nc.scalar.activation(out=pair_buffer("g", i), in_=pair_buffer("pre_og", i, BANK)[:, :, GATE_G], func=ACT.Tanh)

        def gate_o(i):
            nc.scalar.activation(out=pair_buffer("o", i), in_=pair_buffer("pre_og", i, BANK)[:, :, GATE_O], func=ACT.Sigmoid)

        def diff(i):
            gates = pair_buffer("gates_ai", i, BANK)
            engine = nc.gpsimd if i in DIFF_ON_GPSIMD else nc.vector
            engine.tensor_tensor(out=pair_buffer("diff", i), in0=gates[:, :, GATE_I], in1=gates[:, :, ALPHA], op=ALU.subtract)

        def weight(i):
            nc.scalar.activation(out=pair_buffer("w", i), in_=pair_buffer("diff", i), func=ACT.Sigmoid)

        def cell_term(i):
            if i in CELL_ON_GPSIMD:
                nc.gpsimd.tensor_tensor(out=pair_buffer("term", i), in0=pair_buffer("g", i), in1=c_in(i), op=ALU.subtract)
            else:
                nc.vector.scalar_tensor_tensor(
                    out=pair_buffer("term", i), in0=pair_buffer("w", i), scalar=-1.0, in1=c_in(i), op0=ALU.add, op1=ALU.mult
                )

        def cell_product(i):
            engine, factor = (nc.gpsimd, "term") if i in CELL_ON_GPSIMD else (nc.vector, "g")
            engine.tensor_tensor(
                out=pair_buffer("product", i), in0=pair_buffer("w", i), in1=pair_buffer(factor, i), op=ALU.mult
            )

        def cell(i):
            if i in CELL_ON_GPSIMD:
                nc.gpsimd.tensor_tensor(out=pair_buffer("c_1", i), in0=pair_buffer("product", i), in1=c_in(i), op=ALU.add)
            else:
                nc.vector.tensor_tensor(
                    out=pair_buffer("c_1", i), in0=pair_buffer("product", i), in1=pair_buffer("term", i), op=ALU.subtract
                )
            nc.sync.dma_start(out=c_out[:, i : i + 1, :], in_=pair_buffer("c_1", i))

        def tanh_cell(i):
            nc.scalar.activation(out=pair_buffer("tanh_c", i), in_=pair_buffer("c_1", i), func=ACT.Tanh)

        def hidden(i, count=1, engine=nc.vector):
            engine.tensor_tensor(
                out=pair_buffer("h_1", i, count=count),
                in0=pair_buffer("o", i, count=count),
                in1=pair_buffer("tanh_c", i, count=count),
                op=ALU.mult,
            )
            nc.sync.dma_start(out=h_out[:, i : i + count, :], in_=pair_buffer("h_1", i, count=count))

        def run(fn, i, *args):
            if 0 <= i < TILES:
                fn(i, *args)

        transpose_head_state("hT", h_first, 0, nc.scalar.copy)
        open_plain_banks(0)
        weave(plain_og(0))
        transpose_head_state("hT", h_head, 1, nc.vector.tensor_copy)
        transpose_head_state("cT", c_head, 0, nc.scalar.copy)
        weave(plain_i(0))
        spread_bias(bias_og, slice(BANK, 2 * BANK), "state", nc.vector.tensor_copy)
        spread_bias(bias_ai, WHOLE, "tr", nc.scalar.copy)
        weave(plain_alpha(0))
        add_bias(0, "og")
        add_bias(0, "ai")

        def plain_tile(s):
            if s + 2 < PLAIN_HEAD:
                return s + 2
            return s if s >= PLAIN_HEAD else -1

        def plain_and_transposes(s, gaps):
            i = plain_tile(s)
            matmuls = []
            if i >= 0:
                open_plain_banks(i)
                matmuls = plain_og(i) + plain_i(i) + plain_alpha(i)
            transposes = x_transposes(s + 1)
            if s + 1 >= STATE_HEAD and s % 2 == 1:
                transposes = transposes + state_transposes(s + 1)
            weave(matmuls, transposes, gaps)

        for s in range(-1, LAST - 1):
            plain_and_transposes(s, gaps=5)
            run(add_mx, s - 1, "og")
            run(gates_ai, s - 1)
            run(cell, s - 2)
            copy_xT(s + 1, 0)
            run(gate_g, s - 1)
            run(diff, s - 1)
            copy_xT(s + 1, 1)
            run(cell_term, s - 1)
            run(add_bias, plain_tile(s), "og")
            run(add_bias, plain_tile(s), "ai")
            run(weight, s - 1)
            quantize(s + 1)
            if ("stateT", s + 1) in t:
                copy_stateT(s + 1)
            run(tanh_cell, s - 2)
            run(cell_product, s - 1)
            presort(s + 2)
            run(gate_o, s - 1)
            run(mx_ai, s)
            run(mx_og, s)
            run(add_mx, s, "ai")
            if s % 2 == 1:
                run(hidden, s - 3, 2)

        w, x, y, z = LAST - 3, LAST - 2, LAST - 1, LAST
        plain_and_transposes(y, gaps=3)
        add_mx(x, "og")
        gates_ai(x)
        cell(w)
        copy_xT(z, 0)
        copy_xT(z, 1)
        gate_g(x)
        diff(x)
        cell_term(x)
        add_bias(y, "og")
        quantize(z)
        add_bias(y, "ai")
        weight(x)
        tanh_cell(w)
        cell_product(x)
        hidden(w, engine=nc.gpsimd)
        gate_o(x)

        mx_ai(y)
        open_plain_banks(z)
        weave(plain_i(z) + plain_alpha(z))
        mx_gate("ai", z, GATE_I, "state")
        mx_gate("ai", z, ALPHA, "tr")
        add_mx(y, "ai")
        add_bias(z, "ai")
        weave(plain_og(z))
        mx_gate("og", y, GATE_G, "mx_og")
        mx_gate("og", z, GATE_G, "tr")
        mx_gate("og", y, GATE_O, "mx_ai")
        mx_gate("og", z, GATE_O, "plain_ai")

        gates_ai(y)
        cell(x)
        for cols in (GATE_I, ALPHA):
            add_mx(z, "ai", cols)
            gates_ai(z, cols)
        diff(y)
        tanh_cell(x)
        weight(y)
        add_bias(z, "og")
        diff(z)
        add_mx(y, "og", GATE_G)
        gate_g(y)
        add_mx(z, "og", GATE_G)
        weight(z)
        gate_g(z)
        for i in (y, z):
            cell_term(i)
            cell_product(i)
            add_mx(i, "og", GATE_O)
            cell(i)
            gate_o(i)
            tanh_cell(i)
        for i in (x, y, z):
            hidden(i)
